import numpy as np
import ml_dtypes


def mxq(x, axis, fmt="e4m3"):
    dtype, down = {"e4m3": (ml_dtypes.float8_e4m3fn, 7), "e5m2": (ml_dtypes.float8_e5m2, 14)}[fmt]
    v = np.moveaxis(np.asarray(x, np.float32).astype(ml_dtypes.bfloat16).astype(np.float64), axis, -1)
    blocks = v.reshape(v.shape[:-1] + (-1, 32))
    amax = np.abs(blocks).max(-1, keepdims=True)
    byte = np.maximum(np.where(amax > 0, np.frexp(amax)[1] - 1 + 127, 0) - down, 1)
    scale = np.exp2(byte - 127.0)
    codes = (blocks / scale).astype(np.float32).astype(dtype).astype(np.float64)
    return np.moveaxis((codes * scale).reshape(v.shape), -1, axis)


WIDE = False


def mx_kscale(k):
    if not WIDE:
        return np.ones(k)
    levels = np.array([10, -10, 5, -5, 0])
    if k % 512:
        return np.exp2(np.random.permutation(np.resize(levels, k // 32))).repeat(32)
    a = np.empty((k // 512, 16))
    for p in range(k // 512):
        a[p, :8] = np.random.permutation(np.resize(levels, 8))
        for g in range(8):
            far = levels[np.abs(levels - a[p, g]) >= 10]
            a[p, g + 8] = far[np.random.randint(len(far))]
    return np.exp2(a.ravel()).repeat(32)


BF16 = ml_dtypes.bfloat16


def bf(x):
    return np.asarray(x, np.float32).astype(BF16)


def f64(x):
    return np.asarray(x).astype(np.float64)


B, T, N, C, WIN, F = 1, 4, 512, 512, 3, 3
NW = T - WIN + 1


def sigmoid(v):
    return 1.0 / (1.0 + np.exp(-v))


def draw0():
    t = mx_kscale(C)
    return {"agg": bf(np.random.standard_normal((B, NW, N, C)) * t),
            "W": bf(np.random.standard_normal((NW, F, C, 2 * C)) / np.sqrt(C) / t[:, None]),
            "b": bf(np.random.standard_normal((NW, F, 2 * C)) * 0.3)}


def core(agg, W, b):
    pre = (mxq(f64(agg), 3, "e4m3")[:, :, None] @ mxq(f64(W), 2, "e4m3")) + f64(b)[None, :, :, None, :]
    lhs, rhs = pre[..., :C], pre[..., C:]
    glu = lhs * sigmoid(rhs)
    return glu.max(axis=2)


def e4m3fn_bytes(y):
    return np.clip(np.asarray(y, np.float64), -448.0, 448.0).astype(np.float32).astype(ml_dtypes.float8_e4m3fn).view(np.uint8)


def e4m3fn_values(b):
    return np.asarray(b, np.uint8).view(ml_dtypes.float8_e4m3fn).astype(np.float64)


def setup_inputs():
    d = draw0()
    x0 = np.asarray(d['W']).astype(np.float64)
    s = (np.max(np.abs(x0), axis=(0, 1, 3), keepdims=True) / 448.0).astype(np.float32)
    out = {}
    for k, v in d.items():
        if k == 'W':
            out['W_bytes'] = e4m3fn_bytes(x0 / s.astype(np.float64))
            out['W_scale'] = s
        else:
            out[k] = v
    return out


def reference(agg, W_bytes, W_scale, b):
    return core(agg, e4m3fn_values(W_bytes) * W_scale.astype(np.float64), b)

@@ -1,0 +1,254 @@
+from contextlib import ExitStack
+
+import concourse.mybir as mybir
+from concourse.masks import make_identity
+
+F32 = mybir.dt.float32
+BF16 = mybir.dt.bfloat16
+U32 = mybir.dt.uint32
+U8 = mybir.dt.uint8
+FP8 = mybir.dt.float8_e4m3fn
+X4 = mybir.dt.float8_e4m3fn_x4
+ACT = mybir.ActivationFunctionType
+ALU = mybir.AluOpType
+
+P = 128
+NW, NF, N, C = 2, 3, 512, 512
+NB = NW * NF
+FLOPS = 2 * NW * NF * N * C * 2 * C
+
+
+def tile_stsindividuallayer_pb_kernel(tc, agg, W_bytes, W_scale, b, out):
+    nc = tc.nc
+    with ExitStack() as ctx:
+        keep = ctx.enter_context(tc.tile_pool(name="keep", bufs=1))
+        work = ctx.enter_context(tc.tile_pool(name="work", bufs=3))
+        psum = ctx.enter_context(tc.psum_pool(name="psum", bufs=2))
+        ctx.enter_context(tc.manual_schedule())
+
+        zero = keep.tile([P, 1], F32, name="zero")
+        nc.vector.memset(zero[:], 0.0)
+        warm = keep.tile([P, 1], F32, name="warm")
+        nc.scalar.activation(out=warm[:], in_=zero[:], func=ACT.Sigmoid)
+        b_rows = keep.tile([P, P], BF16, name="b_rows")
+        nc.gpsimd.memset(b_rows[:], 0.0)
+        ident_f = keep.tile([P, P], F32, name="ident_f")
+        make_identity(nc, ident_f[:])
+        ident_b = keep.tile([P, P], BF16, name="ident_b")
+        make_identity(nc, ident_b[:])
+
+        sc = keep.tile([P, 4], F32, name="sc")
+        nc.sync.dma_start(out=sc[:], in_=W_scale[0, 0].rearrange("(p t) d -> p (t d)", t=4))
+        wbytes = {}
+        w_view0 = W_bytes[0, 0].rearrange("(p t) n -> p t n", t=4)
+        for t in (0, 2, 1, 3):
+            wb = keep.tile([P, 2 * C], U8, name="wbytes0_%d" % t)
+            nc.sync.dma_start(out=wb[:], in_=w_view0[:, t, :])
+            wbytes[(0, t)] = wb[:]
+        a_sb = []
+
+        def load_agg(w):
+            a = keep.tile([P, 4, C], BF16, name="a_sb%d" % w)
+            nc.sync.dma_start(out=a[:], in_=agg[0, w].rearrange("(i p) k -> p i k", p=P))
+            a_sb.append(a)
+
+        def load_w(blk):
+            w, f = divmod(blk, NF)
+            wb = keep.tile([P, 4, 2 * C], U8, name="wbytes%d" % blk)
+            nc.sync.dma_start(out=wb[:], in_=W_bytes[w, f].rearrange("(p t) n -> p t n", t=4))
+            for t in range(4):
+                wbytes[(blk, t)] = wb[:, t, :]
+
+        load_agg(0)
+        load_w(1)
+        nc.sync.dma_start(out=b_rows[0:48, :], in_=b.rearrange("w f (c p) -> (w f c) p", p=P))
+        load_w(2)
+        load_agg(1)
+        load_w(3)
+        load_w(4)
+        load_w(5)
+
+        wide = {}
+
+        def widen(blk, t, eng):
+            if blk not in wide:
+                wide[blk] = work.tile([P, 4, 2 * C], BF16, tag="wide", bufs=3, name="wide%d" % blk)
+            src = wbytes[(blk, t)].bitcast(FP8)
+            dst = wide[blk][:, t, :]
+            if eng == "S":
+                nc.scalar.activation(out=dst, in_=src, func=ACT.Copy, scale=sc[:, t:t + 1])
+            else:
+                nc.vector.tensor_scalar(out=dst, in0=src, scalar1=sc[:, t:t + 1], scalar2=None, op0=ALU.mult)
+
+        grp = {}
+        codes = {}
+
+        def interleave(blk, j0, nj):
+            g = work.tile([P, 2 * nj * P * 4], BF16, tag="grp", bufs=4, name="grp%d_%d" % (blk, j0), align_bytes=64)
+            src = wide[blk][:].rearrange("p t (h x) -> p t h x", h=2)[:, :, :, P * j0:P * (j0 + nj)]
+            nc.vector.tensor_copy(
+                out=g[:].rearrange("p (h x t) -> p h x t", h=2, t=4),
+                in_=src.rearrange("p t h x -> p h x t"),
+            )
+            grp[(blk, j0)] = g
+
+        def quantize(blk, j0, nj):
+            cd = keep.tile([P, 2 * nj * P], U32, name="wc%d_%d" % (blk, j0), align_bytes=64)
+            sl = keep.tile([P, 2 * nj * P], U8, name="ws%d_%d" % (blk, j0), align_bytes=64)
+            nc.vector.quantize_mx(out=cd[:].bitcast(X4), scales=sl[:], in_=grp[(blk, j0)][:])
+            for j in range(j0, j0 + nj):
+                for h in range(2):
+                    cols = slice((h * nj + j - j0) * P, (h * nj + j - j0 + 1) * P)
+                    codes[(blk, j, h)] = (cd[:, cols], sl[:, cols])
+
+        a_grp = {}
+        a_q = {}
+        xts = {}
+
+        def agg_transposes(w):
+            a_grp[w] = keep.tile([P, 4 * N], BF16, name="a_grp%d" % w, align_bytes=64)
+            for h in range(2):
+                xt = psum.tile([P, 2, 2, P], F32, tag="T", bufs=2, name="xt%d_%d" % (w, h))
+                for i2 in range(2):
+                    words = a_sb[w][:, 2 * h + i2, :].bitcast(F32)
+                    for u in range(2):
+                        nc.tensor.transpose(xt[:, i2, u, :], words[:, u:C // 2:2], ident_f[:])
+                xts[(w, h)] = xt
+
+        def agg_evac(w, h, eng):
+            dst = a_grp[w][:].bitcast(F32)[:, 512 * h:512 * (h + 1)].rearrange("p (i r u) -> p i r u", i=2, u=2)
+            src = xts[(w, h)][:].rearrange("p i u r -> p i r u")
+            if eng == "S":
+                nc.scalar.copy(out=dst, in_=src)
+            else:
+                nc.vector.tensor_copy(out=dst, in_=src)
+
+        def agg_quantize(w):
+            cd = keep.tile([P, N], U32, name="ac%d" % w, align_bytes=64)
+            sl = keep.tile([P, N], U8, name="as%d" % w, align_bytes=64)
+            nc.vector.quantize_mx(out=cd[:].bitcast(X4), scales=sl[:], in_=a_grp[w][:])
+            a_q[w] = (cd, sl)
+
+        bias = keep.tile([P, 48], F32, name="bias")
+        acc = {}
+
+        def mm(s):
+            blk, j = divmod(s, 4)
+            w = blk // NF
+            for h in (1, 0):
+                ps = psum.tile([P, N], F32, tag="LR%d" % h, bufs=3, name="acc%d_%d" % (s, h))
+                cd, sl = codes[(blk, j, h)]
+                nc.tensor.matmul_mx(
+                    out=ps[:], lhsT=cd.bitcast(X4), lhsT_scale=sl,
+                    rhs=a_q[w][0][:].bitcast(X4), rhs_scale=a_q[w][1][:],
+                    start=True, stop=True,
+                )
+                acc[(s, h)] = ps
+
+        sig = {}
+        best = {}
+        glu = {}
+
+        def sigmoid(s):
+            blk, j = divmod(s, 4)
+            sg = work.tile([P, N], F32, tag="sig", bufs=3, name="sig%d" % s)
+            col = blk * 8 + 4 + j
+            nc.scalar.activation(out=sg[:], in_=acc[(s, 1)][:], func=ACT.Sigmoid, bias=bias[:, col:col + 1])
+            sig[s] = sg
+
+        def product(s):
+            blk, j = divmod(s, 4)
+            w, f = divmod(blk, NF)
+            if f == 0:
+                best[(w, j)] = keep.tile([P, N], F32, name="best%d_%d" % (w, j))
+                dst = best[(w, j)]
+            else:
+                dst = work.tile([P, N], F32, tag="glu", bufs=3, name="glu%d" % s)
+                glu[s] = dst
+            col = blk * 8 + j
+            nc.vector.scalar_tensor_tensor(
+                out=dst[:], in0=acc[(s, 0)][:], scalar=bias[:, col:col + 1], in1=sig[s][:],
+                op0=ALU.add, op1=ALU.mult,
+            )
+
+        def merge(s):
+            blk, j = divmod(s, 4)
+            w, f = divmod(blk, NF)
+            if f > 0:
+                nc.vector.tensor_tensor(out=best[(w, j)][:], in0=best[(w, j)][:], in1=glu[s][:], op=ALU.max)
+
+        outT = {}
+
+        def out_transposes(s):
+            blk, j = divmod(s, 4)
+            w = blk // NF
+            ot = psum.tile([P, 4, P], F32, tag="T", bufs=2, name="ot%d" % s)
+            for i in range(4):
+                nc.tensor.transpose(ot[:, i, :], best[(w, j)][:, P * i:P * (i + 1)], ident_f[:])
+            outT[s] = ot
+
+        def out_store(s):
+            blk, j = divmod(s, 4)
+            w = blk // NF
+            o = work.tile([P, 4, P], F32, tag="o", bufs=3, name="o%d" % s)
+            nc.scalar.copy(out=o[:], in_=outT[s][:])
+            nc.sync.dma_start(
+                out=out[0, w].rearrange("(i p) c -> p i c", p=P)[:, :, P * j:P * (j + 1)], in_=o[:]
+            )
+
+        widen(0, 0, "S")
+        widen(0, 2, "V")
+        widen(0, 1, "S")
+        widen(0, 3, "V")
+        agg_transposes(0)
+        agg_evac(0, 0, "V")
+        agg_evac(0, 1, "V")
+        bT = psum.tile([P, P], BF16, tag="T", bufs=2, name="bT")
+        nc.tensor.transpose(bT[:], b_rows[:], ident_b[:])
+        nc.vector.tensor_copy(out=bias[:], in_=bT[:, 0:48])
+        agg_quantize(0)
+        for t in range(4):
+            widen(1, t, "S")
+        interleave(0, 0, 1)
+        interleave(0, 1, 1)
+        quantize(0, 0, 1)
+        interleave(0, 2, 1)
+        quantize(0, 1, 1)
+        interleave(0, 3, 1)
+        quantize(0, 2, 1)
+        quantize(0, 3, 1)
+        mm(0)
+
+        for s in range(4 * NB):
+            blk, j = divmod(s, 4)
+            f = blk % NF
+            if s + 1 < 4 * NB:
+                mm(s + 1)
+            if s >= 1 and ((s - 1) // 4) % NF == 2:
+                out_transposes(s - 1)
+            if s == 4:
+                agg_transposes(1)
+            sigmoid(s)
+            if blk + 2 < NB:
+                widen(blk + 2, j, "S")
+            if s >= 1 and ((s - 1) // 4) % NF == 2:
+                out_store(s - 1)
+            if s == 4:
+                agg_evac(1, 0, "S")
+            if s == 5:
+                agg_evac(1, 1, "S")
+            product(s)
+            if blk + 1 < NB:
+                if j == 0:
+                    interleave(blk + 1, 0, 2)
+                elif j == 1:
+                    interleave(blk + 1, 2, 2)
+                elif j == 2:
+                    quantize(blk + 1, 0, 2)
+                else:
+                    quantize(blk + 1, 2, 2)
+            if s == 7:
+                agg_quantize(1)
+            merge(s)
+        out_transposes(4 * NB - 1)
+        out_store(4 * NB - 1)

@@ -41,7 +41,7 @@ def tile_stsindividuallayer_pb_kernel(tc, agg, W_bytes, W_scale, b, out):
         nc.sync.dma_start(out=sc[:], in_=W_scale[0, 0].rearrange("(p t) d -> p (t d)", t=4))
         wbytes = {}
         w_view0 = W_bytes[0, 0].rearrange("(p t) n -> p t n", t=4)
-        for t in (0, 2, 1, 3):
+        for t in (1, 0, 2, 3):
             wb = keep.tile([P, 2 * C], U8, name="wbytes0_%d" % t)
             nc.sync.dma_start(out=wb[:], in_=w_view0[:, t, :])
             wbytes[(0, t)] = wb[:]
@@ -83,23 +83,27 @@ def tile_stsindividuallayer_pb_kernel(tc, agg, W_bytes, W_scale, b, out):
         grp = {}
         codes = {}
 
-        def interleave(blk, j0, nj):
-            g = work.tile([P, 2 * nj * P * 4], BF16, tag="grp", bufs=4, name="grp%d_%d" % (blk, j0), align_bytes=64)
-            src = wide[blk][:].rearrange("p t (h x) -> p t h x", h=2)[:, :, :, P * j0:P * (j0 + nj)]
-            nc.vector.tensor_copy(
-                out=g[:].rearrange("p (h x t) -> p h x t", h=2, t=4),
-                in_=src.rearrange("p t h x -> p h x t"),
-            )
-            grp[(blk, j0)] = g
+        def interleave(blk, j, eng):
+            if blk not in grp:
+                grp[blk] = work.tile([P, 16 * 2 * P], BF16, tag="grp", bufs=1, name="grp%d" % blk, align_bytes=64)
+            src = wide[blk][:].rearrange("p t (h x) -> p t h x", h=2)[:, :, :, P * j:P * (j + 1)]
+            src = src.rearrange("p t h x -> p h x t")
+            dst = grp[blk][:, 1024 * j:1024 * (j + 1)].rearrange("p (h x t) -> p h x t", h=2, t=4)
+            if eng == "G":
+                nc.gpsimd.tensor_scalar(out=dst, in0=src, scalar1=1.0, scalar2=0.0, op0=ALU.mult, op1=ALU.add)
+            elif eng == "S":
+                nc.scalar.copy(out=dst, in_=src)
+            else:
+                nc.vector.tensor_copy(out=dst, in_=src)
 
-        def quantize(blk, j0, nj):
-            cd = keep.tile([P, 2 * nj * P], U32, name="wc%d_%d" % (blk, j0), align_bytes=64)
-            sl = keep.tile([P, 2 * nj * P], U8, name="ws%d_%d" % (blk, j0), align_bytes=64)
-            nc.vector.quantize_mx(out=cd[:].bitcast(X4), scales=sl[:], in_=grp[(blk, j0)][:])
-            for j in range(j0, j0 + nj):
+        def quantize(blk, hh):
+            cd = keep.tile([P, 4 * P], U32, name="wc%d_%d" % (blk, hh), align_bytes=64)
+            sl = keep.tile([P, 4 * P], U8, name="ws%d_%d" % (blk, hh), align_bytes=64)
+            nc.vector.quantize_mx(out=cd[:].bitcast(X4), scales=sl[:], in_=grp[blk][:, 2048 * hh:2048 * (hh + 1)])
+            for jj in range(2):
                 for h in range(2):
-                    cols = slice((h * nj + j - j0) * P, (h * nj + j - j0 + 1) * P)
-                    codes[(blk, j, h)] = (cd[:, cols], sl[:, cols])
+                    cols = slice((2 * jj + h) * P, (2 * jj + h + 1) * P)
+                    codes[(blk, 2 * hh + jj, h)] = (cd[:, cols], sl[:, cols])
 
         a_grp = {}
         a_q = {}
@@ -108,20 +112,16 @@ def tile_stsindividuallayer_pb_kernel(tc, agg, W_bytes, W_scale, b, out):
         def agg_transposes(w):
             a_grp[w] = keep.tile([P, 4 * N], BF16, name="a_grp%d" % w, align_bytes=64)
             for h in range(2):
-                xt = psum.tile([P, 2, 2, P], F32, tag="T", bufs=2, name="xt%d_%d" % (w, h))
+                xt = psum.tile([P, 2, 2, P], F32, tag="T", bufs=3, name="xt%d_%d" % (w, h))
                 for i2 in range(2):
                     words = a_sb[w][:, 2 * h + i2, :].bitcast(F32)
                     for u in range(2):
                         nc.tensor.transpose(xt[:, i2, u, :], words[:, u:C // 2:2], ident_f[:])
                 xts[(w, h)] = xt
 
-        def agg_evac(w, h, eng):
+        def agg_evac(w, h):
             dst = a_grp[w][:].bitcast(F32)[:, 512 * h:512 * (h + 1)].rearrange("p (i r u) -> p i r u", i=2, u=2)
-            src = xts[(w, h)][:].rearrange("p i u r -> p i r u")
-            if eng == "S":
-                nc.scalar.copy(out=dst, in_=src)
-            else:
-                nc.vector.tensor_copy(out=dst, in_=src)
+            nc.scalar.copy(out=dst, in_=xts[(w, h)][:].rearrange("p i u r -> p i r u"))
 
         def agg_quantize(w):
             cd = keep.tile([P, N], U32, name="ac%d" % w, align_bytes=64)
@@ -132,123 +132,128 @@ def tile_stsindividuallayer_pb_kernel(tc, agg, W_bytes, W_scale, b, out):
         bias = keep.tile([P, 48], F32, name="bias")
         acc = {}
 
-        def mm(s):
+        def mm(s, h):
             blk, j = divmod(s, 4)
             w = blk // NF
-            for h in (1, 0):
-                ps = psum.tile([P, N], F32, tag="LR%d" % h, bufs=3, name="acc%d_%d" % (s, h))
-                cd, sl = codes[(blk, j, h)]
-                nc.tensor.matmul_mx(
-                    out=ps[:], lhsT=cd.bitcast(X4), lhsT_scale=sl,
-                    rhs=a_q[w][0][:].bitcast(X4), rhs_scale=a_q[w][1][:],
-                    start=True, stop=True,
-                )
-                acc[(s, h)] = ps
+            ps = psum.tile([P, N], F32, tag="LR%d" % h, bufs=3 - h, name="acc%d_%d" % (s, h))
+            cd, sl = codes[(blk, j, h)]
+            nc.tensor.matmul_mx(
+                out=ps[:], lhsT=cd.bitcast(X4), lhsT_scale=sl,
+                rhs=a_q[w][0][:].bitcast(X4), rhs_scale=a_q[w][1][:],
+                start=True, stop=True,
+            )
+            acc[(s, h)] = ps
 
         sig = {}
-        best = {}
         glu = {}
+        bestT = {}
+        gluT = {}
 
         def sigmoid(s):
             blk, j = divmod(s, 4)
-            sg = work.tile([P, N], F32, tag="sig", bufs=3, name="sig%d" % s)
+            sg = work.tile([P, N], F32, tag="sig", bufs=4, name="sig%d" % s)
             col = blk * 8 + 4 + j
             nc.scalar.activation(out=sg[:], in_=acc[(s, 1)][:], func=ACT.Sigmoid, bias=bias[:, col:col + 1])
             sig[s] = sg
 
         def product(s):
             blk, j = divmod(s, 4)
-            w, f = divmod(blk, NF)
-            if f == 0:
-                best[(w, j)] = keep.tile([P, N], F32, name="best%d_%d" % (w, j))
-                dst = best[(w, j)]
-            else:
-                dst = work.tile([P, N], F32, tag="glu", bufs=3, name="glu%d" % s)
-                glu[s] = dst
+            g = work.tile([P, N], F32, tag="glu", bufs=4, name="glu%d" % s)
             col = blk * 8 + j
             nc.vector.scalar_tensor_tensor(
-                out=dst[:], in0=acc[(s, 0)][:], scalar=bias[:, col:col + 1], in1=sig[s][:],
+                out=g[:], in0=acc[(s, 0)][:], scalar=bias[:, col:col + 1], in1=sig[s][:],
                 op0=ALU.add, op1=ALU.mult,
             )
+            glu[s] = g
+
+        def turn(s):
+            gt = psum.tile([P, 4, P], F32, tag="T", bufs=3, name="gt%d" % s)
+            for i in range(4):
+                nc.tensor.transpose(gt[:, i, :], glu[s][:, P * i:P * (i + 1)], ident_f[:])
+            gluT[s] = gt
 
         def merge(s):
             blk, j = divmod(s, 4)
             w, f = divmod(blk, NF)
-            if f > 0:
-                nc.vector.tensor_tensor(out=best[(w, j)][:], in0=best[(w, j)][:], in1=glu[s][:], op=ALU.max)
-
-        outT = {}
-
-        def out_transposes(s):
-            blk, j = divmod(s, 4)
-            w = blk // NF
-            ot = psum.tile([P, 4, P], F32, tag="T", bufs=2, name="ot%d" % s)
-            for i in range(4):
-                nc.tensor.transpose(ot[:, i, :], best[(w, j)][:, P * i:P * (i + 1)], ident_f[:])
-            outT[s] = ot
-
-        def out_store(s):
-            blk, j = divmod(s, 4)
-            w = blk // NF
-            o = work.tile([P, 4, P], F32, tag="o", bufs=3, name="o%d" % s)
-            nc.scalar.copy(out=o[:], in_=outT[s][:])
-            nc.sync.dma_start(
-                out=out[0, w].rearrange("(i p) c -> p i c", p=P)[:, :, P * j:P * (j + 1)], in_=o[:]
-            )
+            if f == 0:
+                bestT[(w, j)] = keep.tile([P, 4, P], F32, name="bestT%d_%d" % (w, j))
+                nc.vector.tensor_copy(out=bestT[(w, j)][:], in_=gluT[s][:])
+            else:
+                nc.vector.tensor_tensor(out=bestT[(w, j)][:], in0=gluT[s][:], in1=bestT[(w, j)][:], op=ALU.max)
+            if f == NF - 1:
+                nc.sync.dma_start(
+                    out=out[0, w].rearrange("(i p) c -> p i c", p=P)[:, :, P * j:P * (j + 1)], in_=bestT[(w, j)][:]
+                )
 
         widen(0, 0, "S")
+        widen(0, 1, "V")
         widen(0, 2, "V")
-        widen(0, 1, "S")
         widen(0, 3, "V")
         agg_transposes(0)
-        agg_evac(0, 0, "V")
-        agg_evac(0, 1, "V")
-        bT = psum.tile([P, P], BF16, tag="T", bufs=2, name="bT")
+        bT = psum.tile([P, P], BF16, tag="T", bufs=3, name="bT")
         nc.tensor.transpose(bT[:], b_rows[:], ident_b[:])
-        nc.vector.tensor_copy(out=bias[:], in_=bT[:, 0:48])
-        agg_quantize(0)
-        for t in range(4):
+        interleave(0, 0, "V")
+        interleave(0, 1, "V")
+        agg_evac(0, 0)
+        agg_evac(0, 1)
+        for t in range(3):
             widen(1, t, "S")
-        interleave(0, 0, 1)
-        interleave(0, 1, 1)
-        quantize(0, 0, 1)
-        interleave(0, 2, 1)
-        quantize(0, 1, 1)
-        interleave(0, 3, 1)
-        quantize(0, 2, 1)
-        quantize(0, 3, 1)
-        mm(0)
+        agg_quantize(0)
+        quantize(0, 0)
+        nc.vector.tensor_copy(out=bias[:], in_=bT[:, 0:48])
+        interleave(0, 2, "V")
+        interleave(0, 3, "V")
+        quantize(0, 1)
+        widen(1, 3, "V")
 
-        for s in range(4 * NB):
-            blk, j = divmod(s, 4)
-            f = blk % NF
-            if s + 1 < 4 * NB:
-                mm(s + 1)
-            if s >= 1 and ((s - 1) // 4) % NF == 2:
-                out_transposes(s - 1)
-            if s == 4:
+        for c in range(NB):
+            s0 = 4 * c
+            if c + 1 < NB:
+                for j in range(3):
+                    interleave(c + 1, j, "G")
+            if c > 0:
+                turn(s0 - 1)
+                merge(s0 - 2)
+                merge(s0 - 1)
+            mm(s0, 1)
+            mm(s0, 0)
+            mm(s0 + 1, 1)
+            mm(s0 + 1, 0)
+            sigmoid(s0)
+            sigmoid(s0 + 1)
+            mm(s0 + 2, 1)
+            mm(s0 + 2, 0)
+            sigmoid(s0 + 2)
+            if c == 1:
                 agg_transposes(1)
-            sigmoid(s)
-            if blk + 2 < NB:
-                widen(blk + 2, j, "S")
-            if s >= 1 and ((s - 1) // 4) % NF == 2:
-                out_store(s - 1)
-            if s == 4:
-                agg_evac(1, 0, "S")
-            if s == 5:
-                agg_evac(1, 1, "S")
-            product(s)
-            if blk + 1 < NB:
-                if j == 0:
-                    interleave(blk + 1, 0, 2)
-                elif j == 1:
-                    interleave(blk + 1, 2, 2)
-                elif j == 2:
-                    quantize(blk + 1, 0, 2)
-                else:
-                    quantize(blk + 1, 2, 2)
-            if s == 7:
+                agg_evac(1, 0)
+                agg_evac(1, 1)
+            elif c + 2 < NB:
+                widen(c + 2, 0, "S")
+            mm(s0 + 3, 1)
+            sigmoid(s0 + 3)
+            if c + 2 < NB:
+                for t in range(0 if c == 1 else 1, 4):
+                    widen(c + 2, t, "S")
+            if c == NB - 2:
+                interleave(c + 1, 3, "S")
+            product(s0)
+            turn(s0)
+            mm(s0 + 3, 0)
+            product(s0 + 1)
+            turn(s0 + 1)
+            product(s0 + 2)
+            turn(s0 + 2)
+            merge(s0)
+            product(s0 + 3)
+            merge(s0 + 1)
+            if c == 2:
                 agg_quantize(1)
-            merge(s)
-        out_transposes(4 * NB - 1)
-        out_store(4 * NB - 1)
+            if c + 1 < NB:
+                if c != NB - 2:
+                    interleave(c + 1, 3, "V")
+                quantize(c + 1, 0)
+                quantize(c + 1, 1)
+        turn(4 * NB - 1)
+        merge(4 * NB - 2)
+        merge(4 * NB - 1)

@@ -81,29 +81,30 @@ def tile_stsindividuallayer_pb_kernel(tc, agg, W_bytes, W_scale, b, out):
                 nc.vector.tensor_scalar(out=dst, in0=src, scalar1=sc[:, t:t + 1], scalar2=None, op0=ALU.mult)
 
         grp = {}
-        codes = {}
+        where = {}
+        half = {}
 
-        def interleave(blk, j, eng):
+        def interleave(blk, j0, nj, eng):
             if blk not in grp:
                 grp[blk] = work.tile([P, 16 * 2 * P], BF16, tag="grp", bufs=1, name="grp%d" % blk, align_bytes=64)
-            src = wide[blk][:].rearrange("p t (h x) -> p t h x", h=2)[:, :, :, P * j:P * (j + 1)]
+            src = wide[blk][:].rearrange("p t (h x) -> p t h x", h=2)[:, :, :, P * j0:P * (j0 + nj)]
             src = src.rearrange("p t h x -> p h x t")
-            dst = grp[blk][:, 1024 * j:1024 * (j + 1)].rearrange("p (h x t) -> p h x t", h=2, t=4)
+            dst = grp[blk][:, 1024 * j0:1024 * (j0 + nj)].rearrange("p (h x t) -> p h x t", h=2, t=4)
             if eng == "G":
                 nc.gpsimd.tensor_scalar(out=dst, in0=src, scalar1=1.0, scalar2=0.0, op0=ALU.mult, op1=ALU.add)
             elif eng == "S":
                 nc.scalar.copy(out=dst, in_=src)
             else:
                 nc.vector.tensor_copy(out=dst, in_=src)
+            for j in range(j0, j0 + nj):
+                for h in range(2):
+                    where[(blk, j, h)] = 2 * j0 + h * nj + j - j0
 
         def quantize(blk, hh):
             cd = keep.tile([P, 4 * P], U32, name="wc%d_%d" % (blk, hh), align_bytes=64)
             sl = keep.tile([P, 4 * P], U8, name="ws%d_%d" % (blk, hh), align_bytes=64)
             nc.vector.quantize_mx(out=cd[:].bitcast(X4), scales=sl[:], in_=grp[blk][:, 2048 * hh:2048 * (hh + 1)])
-            for jj in range(2):
-                for h in range(2):
-                    cols = slice((2 * jj + h) * P, (2 * jj + h + 1) * P)
-                    codes[(blk, 2 * hh + jj, h)] = (cd[:, cols], sl[:, cols])
+            half[(blk, hh)] = (cd, sl)
 
         a_grp = {}
         a_q = {}
@@ -136,9 +137,11 @@ def tile_stsindividuallayer_pb_kernel(tc, agg, W_bytes, W_scale, b, out):
             blk, j = divmod(s, 4)
             w = blk // NF
             ps = psum.tile([P, N], F32, tag="LR%d" % h, bufs=3 - h, name="acc%d_%d" % (s, h))
-            cd, sl = codes[(blk, j, h)]
+            slot = where[(blk, j, h)]
+            cd, sl = half[(blk, slot // 4)]
+            cols = slice((slot % 4) * P, (slot % 4 + 1) * P)
             nc.tensor.matmul_mx(
-                out=ps[:], lhsT=cd.bitcast(X4), lhsT_scale=sl,
+                out=ps[:], lhsT=cd[:, cols].bitcast(X4), lhsT_scale=sl[:, cols],
                 rhs=a_q[w][0][:].bitcast(X4), rhs_scale=a_q[w][1][:],
                 start=True, stop=True,
             )
@@ -151,7 +154,7 @@ def tile_stsindividuallayer_pb_kernel(tc, agg, W_bytes, W_scale, b, out):
 
         def sigmoid(s):
             blk, j = divmod(s, 4)
-            sg = work.tile([P, N], F32, tag="sig", bufs=4, name="sig%d" % s)
+            sg = work.tile([P, N], F32, tag="sig", bufs=6, name="sig%d" % s)
             col = blk * 8 + 4 + j
             nc.scalar.activation(out=sg[:], in_=acc[(s, 1)][:], func=ACT.Sigmoid, bias=bias[:, col:col + 1])
             sig[s] = sg
@@ -192,8 +195,8 @@ def tile_stsindividuallayer_pb_kernel(tc, agg, W_bytes, W_scale, b, out):
         agg_transposes(0)
         bT = psum.tile([P, P], BF16, tag="T", bufs=3, name="bT")
         nc.tensor.transpose(bT[:], b_rows[:], ident_b[:])
-        interleave(0, 0, "V")
-        interleave(0, 1, "V")
+        interleave(0, 0, 1, "V")
+        interleave(0, 1, 1, "V")
         agg_evac(0, 0)
         agg_evac(0, 1)
         for t in range(3):
@@ -201,59 +204,64 @@ def tile_stsindividuallayer_pb_kernel(tc, agg, W_bytes, W_scale, b, out):
         agg_quantize(0)
         quantize(0, 0)
         nc.vector.tensor_copy(out=bias[:], in_=bT[:, 0:48])
-        interleave(0, 2, "V")
-        interleave(0, 3, "V")
+        interleave(0, 2, 1, "V")
+        interleave(0, 3, 1, "V")
         quantize(0, 1)
         widen(1, 3, "V")
+        for s in range(2):
+            mm(s, 1)
+            mm(s, 0)
 
         for c in range(NB):
             s0 = 4 * c
             if c + 1 < NB:
-                for j in range(3):
-                    interleave(c + 1, j, "G")
-            if c > 0:
-                turn(s0 - 1)
-                merge(s0 - 2)
-                merge(s0 - 1)
-            mm(s0, 1)
-            mm(s0, 0)
-            mm(s0 + 1, 1)
-            mm(s0 + 1, 0)
+                interleave(c + 1, 0, 3, "G")
             sigmoid(s0)
-            sigmoid(s0 + 1)
             mm(s0 + 2, 1)
-            mm(s0 + 2, 0)
+            sigmoid(s0 + 1)
+            mm(s0 + 3, 1)
             sigmoid(s0 + 2)
+            sigmoid(s0 + 3)
+            if c > 0:
+                merge(s0 - 3)
+                merge(s0 - 2)
             if c == 1:
                 agg_transposes(1)
                 agg_evac(1, 0)
                 agg_evac(1, 1)
-            elif c + 2 < NB:
-                widen(c + 2, 0, "S")
-            mm(s0 + 3, 1)
-            sigmoid(s0 + 3)
             if c + 2 < NB:
-                for t in range(0 if c == 1 else 1, 4):
+                for t in range(4):
                     widen(c + 2, t, "S")
             if c == NB - 2:
-                interleave(c + 1, 3, "S")
+                interleave(c + 1, 3, 1, "S")
+            if c > 0:
+                product(s0 - 1)
+            mm(s0 + 2, 0)
+            if c > 0:
+                turn(s0 - 1)
             product(s0)
-            turn(s0)
             mm(s0 + 3, 0)
+            turn(s0)
             product(s0 + 1)
             turn(s0 + 1)
             product(s0 + 2)
+            if c > 0:
+                merge(s0 - 1)
             turn(s0 + 2)
             merge(s0)
-            product(s0 + 3)
-            merge(s0 + 1)
             if c == 2:
                 agg_quantize(1)
             if c + 1 < NB:
                 if c != NB - 2:
-                    interleave(c + 1, 3, "V")
+                    interleave(c + 1, 3, 1, "V")
                 quantize(c + 1, 0)
                 quantize(c + 1, 1)
-        turn(4 * NB - 1)
-        merge(4 * NB - 2)
-        merge(4 * NB - 1)
+                for s in (s0 + 4, s0 + 5):
+                    mm(s, 1)
+                    mm(s, 0)
+        last = 4 * NB - 1
+        product(last)
+        turn(last)
+        merge(last - 2)
+        merge(last - 1)
+        merge(last)

@@ -110,19 +110,23 @@ def tile_stsindividuallayer_pb_kernel(tc, agg, W_bytes, W_scale, b, out):
         a_q = {}
         xts = {}
 
-        def agg_transposes(w):
+        def agg_transposes(w, tag, bufs):
             a_grp[w] = keep.tile([P, 4 * N], BF16, name="a_grp%d" % w, align_bytes=64)
             for h in range(2):
-                xt = psum.tile([P, 2, 2, P], F32, tag="T", bufs=3, name="xt%d_%d" % (w, h))
+                xt = psum.tile([P, 2, 2, P], F32, tag=tag, bufs=bufs, name="xt%d_%d" % (w, h))
                 for i2 in range(2):
                     words = a_sb[w][:, 2 * h + i2, :].bitcast(F32)
                     for u in range(2):
                         nc.tensor.transpose(xt[:, i2, u, :], words[:, u:C // 2:2], ident_f[:])
                 xts[(w, h)] = xt
 
-        def agg_evac(w, h):
+        def agg_evac(w, h, eng):
             dst = a_grp[w][:].bitcast(F32)[:, 512 * h:512 * (h + 1)].rearrange("p (i r u) -> p i r u", i=2, u=2)
-            nc.scalar.copy(out=dst, in_=xts[(w, h)][:].rearrange("p i u r -> p i r u"))
+            src = xts[(w, h)][:].rearrange("p i u r -> p i r u")
+            if eng == "S":
+                nc.scalar.copy(out=dst, in_=src)
+            else:
+                nc.vector.tensor_copy(out=dst, in_=src)
 
         def agg_quantize(w):
             cd = keep.tile([P, N], U32, name="ac%d" % w, align_bytes=64)
@@ -136,7 +140,7 @@ def tile_stsindividuallayer_pb_kernel(tc, agg, W_bytes, W_scale, b, out):
         def mm(s, h):
             blk, j = divmod(s, 4)
             w = blk // NF
-            ps = psum.tile([P, N], F32, tag="LR%d" % h, bufs=3 - h, name="acc%d_%d" % (s, h))
+            ps = psum.tile([P, N], F32, tag="LR%d" % h, bufs=3, name="acc%d_%d" % (s, h))
             slot = where[(blk, j, h)]
             cd, sl = half[(blk, slot // 4)]
             cols = slice((slot % 4) * P, (slot % 4 + 1) * P)
@@ -170,7 +174,7 @@ def tile_stsindividuallayer_pb_kernel(tc, agg, W_bytes, W_scale, b, out):
             glu[s] = g
 
         def turn(s):
-            gt = psum.tile([P, 4, P], F32, tag="T", bufs=3, name="gt%d" % s)
+            gt = psum.tile([P, 4, P], F32, tag="T", bufs=2, name="gt%d" % s)
             for i in range(4):
                 nc.tensor.transpose(gt[:, i, :], glu[s][:, P * i:P * (i + 1)], ident_f[:])
             gluT[s] = gt
@@ -192,14 +196,14 @@ def tile_stsindividuallayer_pb_kernel(tc, agg, W_bytes, W_scale, b, out):
         widen(0, 1, "V")
         widen(0, 2, "V")
         widen(0, 3, "V")
-        agg_transposes(0)
-        bT = psum.tile([P, P], BF16, tag="T", bufs=3, name="bT")
-        nc.tensor.transpose(bT[:], b_rows[:], ident_b[:])
+        agg_transposes(0, "T", 2)
         interleave(0, 0, 1, "V")
         interleave(0, 1, 1, "V")
-        agg_evac(0, 0)
-        agg_evac(0, 1)
-        for t in range(3):
+        agg_evac(0, 0, "V")
+        agg_evac(0, 1, "V")
+        bT = psum.tile([P, P], BF16, tag="T", bufs=2, name="bT")
+        nc.tensor.transpose(bT[:], b_rows[:], ident_b[:])
+        for t in range(4):
             widen(1, t, "S")
         agg_quantize(0)
         quantize(0, 0)
@@ -207,28 +211,24 @@ def tile_stsindividuallayer_pb_kernel(tc, agg, W_bytes, W_scale, b, out):
         interleave(0, 2, 1, "V")
         interleave(0, 3, 1, "V")
         quantize(0, 1)
-        widen(1, 3, "V")
-        for s in range(2):
-            mm(s, 1)
-            mm(s, 0)
+        mm(0, 1)
+        mm(0, 0)
+        mm(1, 1)
+        mm(1, 0)
+        mm(2, 1)
 
         for c in range(NB):
             s0 = 4 * c
             if c + 1 < NB:
                 interleave(c + 1, 0, 3, "G")
             sigmoid(s0)
-            mm(s0 + 2, 1)
-            sigmoid(s0 + 1)
             mm(s0 + 3, 1)
+            sigmoid(s0 + 1)
             sigmoid(s0 + 2)
             sigmoid(s0 + 3)
             if c > 0:
                 merge(s0 - 3)
                 merge(s0 - 2)
-            if c == 1:
-                agg_transposes(1)
-                agg_evac(1, 0)
-                agg_evac(1, 1)
             if c + 2 < NB:
                 for t in range(4):
                     widen(c + 2, t, "S")
@@ -243,12 +243,16 @@ def tile_stsindividuallayer_pb_kernel(tc, agg, W_bytes, W_scale, b, out):
             mm(s0 + 3, 0)
             turn(s0)
             product(s0 + 1)
-            turn(s0 + 1)
             product(s0 + 2)
             if c > 0:
                 merge(s0 - 1)
-            turn(s0 + 2)
+            turn(s0 + 1)
             merge(s0)
+            turn(s0 + 2)
+            if c == 0:
+                agg_transposes(1, "LR1", 3)
+                agg_evac(1, 0, "S")
+                agg_evac(1, 1, "S")
             if c == 2:
                 agg_quantize(1)
             if c + 1 < NB:
@@ -256,12 +260,14 @@ def tile_stsindividuallayer_pb_kernel(tc, agg, W_bytes, W_scale, b, out):
                     interleave(c + 1, 3, 1, "V")
                 quantize(c + 1, 0)
                 quantize(c + 1, 1)
-                for s in (s0 + 4, s0 + 5):
-                    mm(s, 1)
-                    mm(s, 0)
+                mm(s0 + 4, 1)
+                mm(s0 + 4, 0)
+                mm(s0 + 5, 1)
+                mm(s0 + 5, 0)
+                mm(s0 + 6, 1)
         last = 4 * NB - 1
         product(last)
-        turn(last)
         merge(last - 2)
+        turn(last)
         merge(last - 1)
         merge(last)

@@ -228,7 +228,6 @@ def tile_stsindividuallayer_pb_kernel(tc, agg, W_bytes, W_scale, b, out):
             sigmoid(s0 + 3)
             if c > 0:
                 merge(s0 - 3)
-                merge(s0 - 2)
             if c + 2 < NB:
                 for t in range(4):
                     widen(c + 2, t, "S")
@@ -239,21 +238,23 @@ def tile_stsindividuallayer_pb_kernel(tc, agg, W_bytes, W_scale, b, out):
             mm(s0 + 2, 0)
             if c > 0:
                 turn(s0 - 1)
+                merge(s0 - 2)
+            else:
+                agg_transposes(1, "LR1", 3)
             product(s0)
-            mm(s0 + 3, 0)
             turn(s0)
+            mm(s0 + 3, 0)
             product(s0 + 1)
             product(s0 + 2)
             if c > 0:
                 merge(s0 - 1)
+            else:
+                agg_evac(1, 0, "V")
+                agg_evac(1, 1, "V")
             turn(s0 + 1)
             merge(s0)
             turn(s0 + 2)
-            if c == 0:
-                agg_transposes(1, "LR1", 3)
-                agg_evac(1, 0, "S")
-                agg_evac(1, 1, "S")
-            if c == 2:
+            if c == 1:
                 agg_quantize(1)
             if c + 1 < NB:
                 if c != NB - 2:

@@ -40,11 +40,16 @@ def tile_stsindividuallayer_pb_kernel(tc, agg, W_bytes, W_scale, b, out):
         sc = keep.tile([P, 4], F32, name="sc")
         nc.sync.dma_start(out=sc[:], in_=W_scale[0, 0].rearrange("(p t) d -> p (t d)", t=4))
         wbytes = {}
-        w_view0 = W_bytes[0, 0].rearrange("(p t) n -> p t n", t=4)
+
+        def load_plane(blk, t):
+            w, f = divmod(blk, NF)
+            wb = keep.tile([P, 2 * C], U8, name="wbytes%d_%d" % (blk, t))
+            nc.sync.dma_start(out=wb[:], in_=W_bytes[w, f].rearrange("(p t) n -> p t n", t=4)[:, t, :])
+            wbytes[(blk, t)] = wb[:]
+
         for t in (1, 0, 2, 3):
-            wb = keep.tile([P, 2 * C], U8, name="wbytes0_%d" % t)
-            nc.sync.dma_start(out=wb[:], in_=w_view0[:, t, :])
-            wbytes[(0, t)] = wb[:]
+            load_plane(0, t)
+        load_plane(1, 0)
         a_sb = []
 
         def load_agg(w):
@@ -60,7 +65,8 @@ def tile_stsindividuallayer_pb_kernel(tc, agg, W_bytes, W_scale, b, out):
                 wbytes[(blk, t)] = wb[:, t, :]
 
         load_agg(0)
-        load_w(1)
+        for t in (1, 2, 3):
+            load_plane(1, t)
         nc.sync.dma_start(out=b_rows[0:48, :], in_=b.rearrange("w f (c p) -> (w f c) p", p=P))
         load_w(2)
         load_agg(1)
@@ -72,7 +78,7 @@ def tile_stsindividuallayer_pb_kernel(tc, agg, W_bytes, W_scale, b, out):
 
         def widen(blk, t, eng):
             if blk not in wide:
-                wide[blk] = work.tile([P, 4, 2 * C], BF16, tag="wide", bufs=3, name="wide%d" % blk)
+                wide[blk] = keep.tile([P, 4, 2 * C], BF16, name="wide%d" % blk)
             src = wbytes[(blk, t)].bitcast(FP8)
             dst = wide[blk][:, t, :]
             if eng == "S":
@@ -81,12 +87,11 @@ def tile_stsindividuallayer_pb_kernel(tc, agg, W_bytes, W_scale, b, out):
                 nc.vector.tensor_scalar(out=dst, in0=src, scalar1=sc[:, t:t + 1], scalar2=None, op0=ALU.mult)
 
         grp = {}
-        where = {}
         half = {}
 
         def interleave(blk, j0, nj, eng):
             if blk not in grp:
-                grp[blk] = work.tile([P, 16 * 2 * P], BF16, tag="grp", bufs=1, name="grp%d" % blk, align_bytes=64)
+                grp[blk] = work.tile([P, 16 * 2 * P], BF16, tag="grp", bufs=GRP_BUFS, name="grp%d" % blk, align_bytes=64)
             src = wide[blk][:].rearrange("p t (h x) -> p t h x", h=2)[:, :, :, P * j0:P * (j0 + nj)]
             src = src.rearrange("p t h x -> p h x t")
             dst = grp[blk][:, 1024 * j0:1024 * (j0 + nj)].rearrange("p (h x t) -> p h x t", h=2, t=4)
@@ -96,9 +101,6 @@ def tile_stsindividuallayer_pb_kernel(tc, agg, W_bytes, W_scale, b, out):
                 nc.scalar.copy(out=dst, in_=src)
             else:
                 nc.vector.tensor_copy(out=dst, in_=src)
-            for j in range(j0, j0 + nj):
-                for h in range(2):
-                    where[(blk, j, h)] = 2 * j0 + h * nj + j - j0
 
         def quantize(blk, hh):
             cd = keep.tile([P, 4 * P], U32, name="wc%d_%d" % (blk, hh), align_bytes=64)
@@ -110,15 +112,15 @@ def tile_stsindividuallayer_pb_kernel(tc, agg, W_bytes, W_scale, b, out):
         a_q = {}
         xts = {}
 
-        def agg_transposes(w, tag, bufs):
-            a_grp[w] = keep.tile([P, 4 * N], BF16, name="a_grp%d" % w, align_bytes=64)
-            for h in range(2):
-                xt = psum.tile([P, 2, 2, P], F32, tag=tag, bufs=bufs, name="xt%d_%d" % (w, h))
-                for i2 in range(2):
-                    words = a_sb[w][:, 2 * h + i2, :].bitcast(F32)
-                    for u in range(2):
-                        nc.tensor.transpose(xt[:, i2, u, :], words[:, u:C // 2:2], ident_f[:])
-                xts[(w, h)] = xt
+        def agg_transposes(w, h, tag, bufs):
+            if w not in a_grp:
+                a_grp[w] = keep.tile([P, 4 * N], BF16, name="a_grp%d" % w, align_bytes=64)
+            xt = psum.tile([P, 2, 2, P], F32, tag=tag, bufs=bufs, name="xt%d_%d" % (w, h))
+            for i2 in range(2):
+                words = a_sb[w][:, 2 * h + i2, :].bitcast(F32)
+                for u in range(2):
+                    nc.tensor.transpose(xt[:, i2, u, :], words[:, u:C // 2:2], ident_f[:])
+            xts[(w, h)] = xt
 
         def agg_evac(w, h, eng):
             dst = a_grp[w][:].bitcast(F32)[:, 512 * h:512 * (h + 1)].rearrange("p (i r u) -> p i r u", i=2, u=2)
@@ -135,12 +137,25 @@ def tile_stsindividuallayer_pb_kernel(tc, agg, W_bytes, W_scale, b, out):
             a_q[w] = (cd, sl)
 
         bias = keep.tile([P, 48], F32, name="bias")
+        bTs = []
+
+        def bias_turn():
+            bT = psum.tile([P, P], BF16, tag="T", bufs=T_BUFS, name="bT")
+            nc.tensor.transpose(bT[:], b_rows[:], ident_b[:])
+            bTs.append(bT)
+
+        def bias_copy(eng):
+            if eng == "S":
+                nc.scalar.copy(out=bias[:], in_=bTs[0][:, 0:48])
+            else:
+                nc.vector.tensor_copy(out=bias[:], in_=bTs[0][:, 0:48])
+
         acc = {}
 
         def mm(s, h):
             blk, j = divmod(s, 4)
             w = blk // NF
-            ps = psum.tile([P, N], F32, tag="LR%d" % h, bufs=3, name="acc%d_%d" % (s, h))
+            ps = psum.tile([P, N], F32, tag="LR%d" % h, bufs=LR_BUFS[h], name="acc%d_%d" % (s, h))
             slot = where[(blk, j, h)]
             cd, sl = half[(blk, slot // 4)]
             cols = slice((slot % 4) * P, (slot % 4 + 1) * P)
@@ -158,14 +173,14 @@ def tile_stsindividuallayer_pb_kernel(tc, agg, W_bytes, W_scale, b, out):
 
         def sigmoid(s):
             blk, j = divmod(s, 4)
-            sg = work.tile([P, N], F32, tag="sig", bufs=6, name="sig%d" % s)
+            sg = work.tile([P, N], F32, tag="sig", bufs=SIG_BUFS, name="sig%d" % s)
             col = blk * 8 + 4 + j
             nc.scalar.activation(out=sg[:], in_=acc[(s, 1)][:], func=ACT.Sigmoid, bias=bias[:, col:col + 1])
             sig[s] = sg
 
         def product(s):
             blk, j = divmod(s, 4)
-            g = work.tile([P, N], F32, tag="glu", bufs=4, name="glu%d" % s)
+            g = work.tile([P, N], F32, tag="glu", bufs=GLU_BUFS, name="glu%d" % s)
             col = blk * 8 + j
             nc.vector.scalar_tensor_tensor(
                 out=g[:], in0=acc[(s, 0)][:], scalar=bias[:, col:col + 1], in1=sig[s][:],
@@ -174,17 +189,20 @@ def tile_stsindividuallayer_pb_kernel(tc, agg, W_bytes, W_scale, b, out):
             glu[s] = g
 
         def turn(s):
-            gt = psum.tile([P, 4, P], F32, tag="T", bufs=2, name="gt%d" % s)
+            gt = psum.tile([P, 4, P], F32, tag=T_TAG(s)[0], bufs=T_TAG(s)[1], name="gt%d" % s)
             for i in range(4):
                 nc.tensor.transpose(gt[:, i, :], glu[s][:, P * i:P * (i + 1)], ident_f[:])
             gluT[s] = gt
 
-        def merge(s):
+        def merge(s, eng):
             blk, j = divmod(s, 4)
             w, f = divmod(blk, NF)
             if f == 0:
                 bestT[(w, j)] = keep.tile([P, 4, P], F32, name="bestT%d_%d" % (w, j))
-                nc.vector.tensor_copy(out=bestT[(w, j)][:], in_=gluT[s][:])
+                if eng == "S":
+                    nc.scalar.copy(out=bestT[(w, j)][:], in_=gluT[s][:])
+                else:
+                    nc.vector.tensor_copy(out=bestT[(w, j)][:], in_=gluT[s][:])
             else:
                 nc.vector.tensor_tensor(out=bestT[(w, j)][:], in0=gluT[s][:], in1=bestT[(w, j)][:], op=ALU.max)
             if f == NF - 1:
@@ -192,83 +210,142 @@ def tile_stsindividuallayer_pb_kernel(tc, agg, W_bytes, W_scale, b, out):
                     out=out[0, w].rearrange("(i p) c -> p i c", p=P)[:, :, P * j:P * (j + 1)], in_=bestT[(w, j)][:]
                 )
 
-        widen(0, 0, "S")
-        widen(0, 1, "V")
-        widen(0, 2, "V")
-        widen(0, 3, "V")
-        agg_transposes(0, "T", 2)
-        interleave(0, 0, 1, "V")
-        interleave(0, 1, 1, "V")
-        agg_evac(0, 0, "V")
-        agg_evac(0, 1, "V")
-        bT = psum.tile([P, P], BF16, tag="T", bufs=2, name="bT")
-        nc.tensor.transpose(bT[:], b_rows[:], ident_b[:])
-        for t in range(4):
-            widen(1, t, "S")
-        agg_quantize(0)
-        quantize(0, 0)
-        nc.vector.tensor_copy(out=bias[:], in_=bT[:, 0:48])
-        interleave(0, 2, 1, "V")
-        interleave(0, 3, 1, "V")
-        quantize(0, 1)
-        mm(0, 1)
-        mm(0, 0)
-        mm(1, 1)
-        mm(1, 0)
-        mm(2, 1)
+        GRP_BUFS, T_BUFS, SIG_BUFS, GLU_BUFS = 1, 2, 6, 4
+        LR_BUFS = (3, 3)
+        WD = {(blk, t): "S" for blk in range(NB) for t in range(4)}
+        for t in (1, 2, 3):
+            WD[(0, t)] = "V"
+        PARTS = {blk: [(0, 3, "G"), (3, 1, "V")] for blk in range(NB)}
+        PARTS[0] = [(j, 1, "V") for j in range(4)]
+        PARTS[NB - 1] = [(0, 3, "G"), (3, 1, "S")]
+        AT_TAG = {0: ("T", 2), 1: ("LR1", 3)}
+        AE = {0: "V", 1: "V"}
+        BC = "V"
+        CPS = ()
+        AHEAD = 1
+        OWN_AFTER = 2
+        SORDER = lambda g, m: [m[0], g[0], g[1], m[1], g[2], g[3], m[2]]
+        T_TAG = lambda s: ("LR1", 3) if s in (21, 23) else ("T", 2)
+        IL_AT = 9
+        ops = {}
+        where = {}
+        queues = {"V": [], "S": [], "G": [], "T": []}
 
-        for c in range(NB):
+        def put(name, eng, fn, args, needs, tag=None, bufs=0, users=()):
+            ops[name] = (fn, args, needs, tag, bufs, users)
+
+        for blk in range(NB):
+            for t in range(4):
+                put(("Wd", blk, t), WD[(blk, t)], widen, (blk, t, WD[(blk, t)]), [])
+            first = True
+            for (j0, nj, eng) in PARTS[blk]:
+                put(("IL", blk, j0), eng, interleave, (blk, j0, nj, eng), [("Wd", blk, t) for t in range(4)],
+                    "grp" if first else None, GRP_BUFS, [("Q", blk, 0), ("Q", blk, 1)])
+                first = False
+                for j in range(j0, j0 + nj):
+                    for h in range(2):
+                        where[(blk, j, h)] = 2 * j0 + h * nj + j - j0
+            for hh in range(2):
+                put(("Q", blk, hh), "V", quantize, (blk, hh),
+                    [("IL", blk, j0) for (j0, nj, eng) in PARTS[blk] if j0 < 2 * hh + 2 and j0 + nj > 2 * hh])
+        for w in range(NW):
+            for h in range(2):
+                put(("AT", w, h), "T", agg_transposes, (w, h) + AT_TAG[w], [], AT_TAG[w][0], AT_TAG[w][1], [("AE", w, h)])
+                put(("AE", w, h), AE[w], agg_evac, (w, h, AE[w]), [("AT", w, h)])
+            put(("AQ", w), "V", agg_quantize, (w,), [("AE", w, 0), ("AE", w, 1)])
+        put(("BT",), "T", bias_turn, (), [], "T", T_BUFS, [("BC",)])
+        put(("BC",), BC, bias_copy, (BC,), [("BT",)])
+        for s in range(4 * NB):
+            blk, j = divmod(s, 4)
+            f = blk % NF
+            for h in range(2):
+                put(("MM", s, h), "T", mm, (s, h), [("Q", blk, where[(blk, j, h)] // 4), ("AQ", blk // NF)],
+                    "LR%d" % h, LR_BUFS[h], [("SG", s) if h else ("PR", s)])
+            put(("SG", s), "S", sigmoid, (s,), [("MM", s, 1), ("BC",)], "sig", SIG_BUFS, [("PR", s)])
+            put(("PR", s), "V", product, (s,), [("MM", s, 0), ("SG", s)], "glu", GLU_BUFS, [("TR", s)])
+            put(("TR", s), "T", turn, (s,), [("PR", s)], T_TAG(s)[0], T_TAG(s)[1], [("MG", s)])
+            put(("MG", s), "V", merge, (s, "S" if s in CPS else "V"), [("TR", s)] + ([("MG", s - 4)] if f else []))
+
+        V, S, G, T = queues["V"], queues["S"], queues["G"], queues["T"]
+        V.extend([("Wd", 0, 1), ("Wd", 0, 2), ("Wd", 0, 3), ("IL", 0, 0), ("IL", 0, 1), ("AE", 0, 0), ("AE", 0, 1), ("AQ", 0), ("Q", 0, 0),
+                  ("BC",), ("IL", 0, 2), ("IL", 0, 3), ("Q", 0, 1)])
+        planes = [("Wd", blk, t) for blk in range(1, NB) for t in range(4) if WD[(blk, t)] == "S"]
+        S.append(("Wd", 0, 0))
+        S.extend(planes[:4 + AHEAD])
+        planes = planes[4 + AHEAD:]
+        T.extend([("AT", 0, 0), ("AT", 0, 1), ("BT",), ("MM", 0, 1), ("MM", 0, 0), ("MM", 1, 1), ("MM", 1, 0), ("MM", 2, 1)])
+        for c in range(NB - 1):
             s0 = 4 * c
             if c + 1 < NB:
-                interleave(c + 1, 0, 3, "G")
-            sigmoid(s0)
-            mm(s0 + 3, 1)
-            sigmoid(s0 + 1)
-            sigmoid(s0 + 2)
-            sigmoid(s0 + 3)
-            if c > 0:
-                merge(s0 - 3)
-            if c + 2 < NB:
-                for t in range(4):
-                    widen(c + 2, t, "S")
-            if c == NB - 2:
-                interleave(c + 1, 3, 1, "S")
-            if c > 0:
-                product(s0 - 1)
-            mm(s0 + 2, 0)
-            if c > 0:
-                turn(s0 - 1)
-                merge(s0 - 2)
-            else:
-                agg_transposes(1, "LR1", 3)
-            product(s0)
-            turn(s0)
-            mm(s0 + 3, 0)
-            product(s0 + 1)
-            product(s0 + 2)
-            if c > 0:
-                merge(s0 - 1)
-            else:
-                agg_evac(1, 0, "V")
-                agg_evac(1, 1, "V")
-            turn(s0 + 1)
-            merge(s0)
-            turn(s0 + 2)
-            if c == 1:
-                agg_quantize(1)
+                G.extend([("IL", c + 1, j0) for (j0, nj, e) in PARTS[c + 1] if e == "G"])
+            early = [("MG", s) for s in (s0 - 3, s0 - 2, s0 - 1) if s in CPS]
+            sgs = [("SG", s0 + j) for j in range(4)]
+            S.extend(SORDER(sgs, early) if early else sgs)
+            fill = planes[:4]
+            planes = planes[4:]
             if c + 1 < NB:
-                if c != NB - 2:
-                    interleave(c + 1, 3, 1, "V")
-                quantize(c + 1, 0)
-                quantize(c + 1, 1)
-                mm(s0 + 4, 1)
-                mm(s0 + 4, 0)
-                mm(s0 + 5, 1)
-                mm(s0 + 5, 0)
-                mm(s0 + 6, 1)
-        last = 4 * NB - 1
-        product(last)
-        merge(last - 2)
-        turn(last)
-        merge(last - 1)
-        merge(last)
+                fill = fill[:IL_AT] + [("IL", c + 1, j0) for (j0, nj, e) in PARTS[c + 1] if e == "S"] + fill[IL_AT:]
+            own = [("MG", s0)] if s0 in CPS else []
+            if c == 0 and AE[1] == "S":
+                own = [("AE", 1, 0), ("AE", 1, 1)] + own
+            k = OWN_AFTER
+            S.extend(fill[:k] + own + fill[k:])
+            vq = []
+            if c > 0:
+                vq.extend([("MG", s0 - 3), ("PR", s0 - 1), ("MG", s0 - 2)])
+            vq.extend([("PR", s0), ("PR", s0 + 1), ("PR", s0 + 2)])
+            if c > 0:
+                vq.append(("MG", s0 - 1))
+            elif AE[1] == "V":
+                vq.extend([("AE", 1, 0), ("AE", 1, 1)])
+            vq.append(("MG", s0))
+            V.extend([x for x in vq if x[0] != "MG" or x[1] not in CPS])
+            if c == 1:
+                V.append(("AQ", 1))
+            if c + 1 < NB:
+                V.extend([("IL", c + 1, j0) for (j0, nj, e) in PARTS[c + 1] if e == "V"])
+                V.extend([("Q", c + 1, 0), ("Q", c + 1, 1)])
+            if c + 2 < NB:
+                V.extend([("Wd", c + 2, t) for t in range(4) if WD[(c + 2, t)] == "V"])
+            T.extend([("MM", s0 + 3, 1), ("MM", s0 + 2, 0)])
+            if c > 0:
+                T.append(("TR", s0 - 1))
+            else:
+                T.extend([("AT", 1, 0), ("AT", 1, 1)])
+            T.extend([("TR", s0), ("MM", s0 + 3, 0), ("TR", s0 + 1), ("TR", s0 + 2)])
+            if c + 1 < NB:
+                T.extend([("MM", s0 + 4, 1), ("MM", s0 + 4, 0), ("MM", s0 + 5, 1), ("MM", s0 + 5, 0), ("MM", s0 + 6, 1)])
+        S.extend([("SG", 20), ("SG", 21), ("SG", 22), ("SG", 23)])
+        V.extend([("MG", 17), ("PR", 19), ("MG", 18), ("PR", 20), ("PR", 21), ("PR", 22), ("MG", 19), ("PR", 23), ("MG", 20), ("MG", 21), ("MG", 22), ("MG", 23)])
+        T.extend([("MM", 23, 1), ("MM", 22, 0), ("TR", 19), ("TR", 20), ("MM", 23, 0), ("TR", 21), ("TR", 22), ("TR", 23)])
+        done = set()
+        handed = {}
+
+        def ready(name):
+            fn, args, needs, tag, bufs, users = ops[name]
+            if any(x not in done for x in needs):
+                return False
+            if tag:
+                lst = handed.setdefault(tag, [])
+                if len(lst) >= bufs and any(x not in done for x in lst[len(lst) - bufs]):
+                    return False
+            return True
+
+        at = {"T": 0, "S": 0, "V": 0, "G": 0}
+        left = sum(len(queues[e]) for e in at)
+        assert left == len(ops), (left, len(ops))
+        while left:
+            moved = 0
+            for e in ("T", "S", "V", "G"):
+                q = queues[e]
+                while at[e] < len(q) and ready(q[at[e]]):
+                    name = q[at[e]]
+                    at[e] += 1
+                    fn, args, needs, tag, bufs, users = ops[name]
+                    if tag:
+                        handed[tag].append(list(users))
+                    fn(*args)
+                    done.add(name)
+                    moved += 1
+            assert moved, [queues[e][at[e]] for e in at if at[e] < len(queues[e])]
+            left -= moved

@@ -89,12 +89,18 @@ def tile_stsindividuallayer_pb_kernel(tc, agg, W_bytes, W_scale, b, out):
         grp = {}
         half = {}
 
-        def interleave(blk, j0, nj, eng):
-            if blk not in grp:
-                grp[blk] = work.tile([P, 16 * 2 * P], BF16, tag="grp", bufs=GRP_BUFS, name="grp%d" % blk, align_bytes=64)
-            src = wide[blk][:].rearrange("p t (h x) -> p t h x", h=2)[:, :, :, P * j0:P * (j0 + nj)]
-            src = src.rearrange("p t h x -> p h x t")
-            dst = grp[blk][:, 1024 * j0:1024 * (j0 + nj)].rearrange("p (h x t) -> p h x t", h=2, t=4)
+        def interleave(blk, s0, ns, eng):
+            hh = s0 // 4
+            if (blk, hh) not in grp:
+                grp[(blk, hh)] = work.tile([P, 16 * P], BF16, tag="grp%d" % hh, bufs=GRP_BUFS, name="grp%d_%d" % (blk, hh), align_bytes=64)
+            src = wide[blk][:, :, P * s0:P * (s0 + ns)]
+            dst = grp[(blk, hh)][:, 4 * P * (s0 - 4 * hh):4 * P * (s0 - 4 * hh + ns)]
+            if FAST:
+                src = src.rearrange("p t (c i) -> p c t i", i=4)
+                dst = dst.rearrange("p (c i t) -> p c t i", i=4, t=4)
+            else:
+                src = src.rearrange("p t x -> p x t")
+                dst = dst.rearrange("p (x t) -> p x t", t=4)
             if eng == "G":
                 nc.gpsimd.tensor_scalar(out=dst, in0=src, scalar1=1.0, scalar2=0.0, op0=ALU.mult, op1=ALU.add)
             elif eng == "S":
@@ -102,11 +108,12 @@ def tile_stsindividuallayer_pb_kernel(tc, agg, W_bytes, W_scale, b, out):
             else:
                 nc.vector.tensor_copy(out=dst, in_=src)
 
-        def quantize(blk, hh):
-            cd = keep.tile([P, 4 * P], U32, name="wc%d_%d" % (blk, hh), align_bytes=64)
-            sl = keep.tile([P, 4 * P], U8, name="ws%d_%d" % (blk, hh), align_bytes=64)
-            nc.vector.quantize_mx(out=cd[:].bitcast(X4), scales=sl[:], in_=grp[blk][:, 2048 * hh:2048 * (hh + 1)])
-            half[(blk, hh)] = (cd, sl)
+        def quantize(blk, i):
+            s0, ns = QS[blk][i]
+            cd = keep.tile([P, ns * P], U32, name="wc%d_%d" % (blk, i), align_bytes=64)
+            sl = keep.tile([P, ns * P], U8, name="ws%d_%d" % (blk, i), align_bytes=64)
+            nc.vector.quantize_mx(out=cd[:].bitcast(X4), scales=sl[:], in_=grp[(blk, s0 // 4)][:, 4 * P * (s0 % 4):4 * P * (s0 % 4 + ns)])
+            half[(blk, i)] = (cd, sl)
 
         a_grp = {}
         a_q = {}
@@ -156,9 +163,9 @@ def tile_stsindividuallayer_pb_kernel(tc, agg, W_bytes, W_scale, b, out):
             blk, j = divmod(s, 4)
             w = blk // NF
             ps = psum.tile([P, N], F32, tag="LR%d" % h, bufs=LR_BUFS[h], name="acc%d_%d" % (s, h))
-            slot = where[(blk, j, h)]
-            cd, sl = half[(blk, slot // 4)]
-            cols = slice((slot % 4) * P, (slot % 4 + 1) * P)
+            i, k = where[(blk, j, h)]
+            cd, sl = half[(blk, i)]
+            cols = slice(k * P, (k + 1) * P)
             nc.tensor.matmul_mx(
                 out=ps[:], lhsT=cd[:, cols].bitcast(X4), lhsT_scale=sl[:, cols],
                 rhs=a_q[w][0][:].bitcast(X4), rhs_scale=a_q[w][1][:],
@@ -212,21 +219,23 @@ def tile_stsindividuallayer_pb_kernel(tc, agg, W_bytes, W_scale, b, out):
 
         GRP_BUFS, T_BUFS, SIG_BUFS, GLU_BUFS = 1, 2, 6, 4
         LR_BUFS = (3, 3)
+        FAST = False
         WD = {(blk, t): "S" for blk in range(NB) for t in range(4)}
         for t in (1, 2, 3):
             WD[(0, t)] = "V"
-        PARTS = {blk: [(0, 3, "G"), (3, 1, "V")] for blk in range(NB)}
-        PARTS[0] = [(j, 1, "V") for j in range(4)]
-        PARTS[NB - 1] = [(0, 3, "G"), (3, 1, "S")]
+        PARTS = {blk: [(4, 4, "G"), (2, 2, "G"), (0, 2, "V")] for blk in range(NB)}
+        PARTS[0] = [(4, 2, "V"), (0, 2, "V"), (6, 2, "V"), (2, 2, "V")]
+        PARTS[NB - 1] = [(4, 4, "G"), (2, 2, "G"), (0, 2, "S")]
         AT_TAG = {0: ("T", 2), 1: ("LR1", 3)}
         AE = {0: "V", 1: "V"}
         BC = "V"
         CPS = ()
         AHEAD = 1
-        OWN_AFTER = 2
-        SORDER = lambda g, m: [m[0], g[0], g[1], m[1], g[2], g[3], m[2]]
+        HEAD_V = [("IL", 0, 4), ("IL", 0, 0), ("AE", 0, 0), ("AE", 0, 1), ("AQ", 0), ("Q", 0, 0), ("Q", 0, 1), ("BC",), ("IL", 0, 6), ("IL", 0, 2), ("Q", 0, 2), ("Q", 0, 3)]
+        NEXT_MM = lambda s: ([("MM", s, 1), ("MM", s + 1, 1), ("MM", s + 2, 1), ("MM", s, 0), ("MM", s + 1, 0)] if s else [("MM", 0, 1), ("MM", 1, 1), ("MM", 0, 0), ("MM", 1, 0), ("MM", 2, 1)])
+        QS = {blk: [(0, 4), (4, 4)] for blk in range(NB)}
+        QS[0] = [(4, 2), (0, 2), (6, 2), (2, 2)]
         T_TAG = lambda s: ("LR1", 3) if s in (21, 23) else ("T", 2)
-        IL_AT = 9
         ops = {}
         where = {}
         queues = {"V": [], "S": [], "G": [], "T": []}
@@ -237,17 +246,19 @@ def tile_stsindividuallayer_pb_kernel(tc, agg, W_bytes, W_scale, b, out):
         for blk in range(NB):
             for t in range(4):
                 put(("Wd", blk, t), WD[(blk, t)], widen, (blk, t, WD[(blk, t)]), [])
-            first = True
+            seen = set()
             for (j0, nj, eng) in PARTS[blk]:
-                put(("IL", blk, j0), eng, interleave, (blk, j0, nj, eng), [("Wd", blk, t) for t in range(4)],
-                    "grp" if first else None, GRP_BUFS, [("Q", blk, 0), ("Q", blk, 1)])
-                first = False
-                for j in range(j0, j0 + nj):
-                    for h in range(2):
-                        where[(blk, j, h)] = 2 * j0 + h * nj + j - j0
-            for hh in range(2):
-                put(("Q", blk, hh), "V", quantize, (blk, hh),
-                    [("IL", blk, j0) for (j0, nj, eng) in PARTS[blk] if j0 < 2 * hh + 2 and j0 + nj > 2 * hh])
+                put(("IL", blk, j0), eng, interleave, (blk, j0, nj, eng),
+                    [("Wd", blk, t) for t in range(4)] + [("IL", blk - 1, x[0]) for x in PARTS.get(blk - 1, []) if x[0] // 4 == j0 // 4],
+                    None if j0 // 4 in seen else "grp%d" % (j0 // 4), GRP_BUFS,
+                    [("Q", blk, i) for i in range(len(QS[blk])) if QS[blk][i][0] // 4 == j0 // 4])
+                seen.add(j0 // 4)
+            for i in range(len(QS[blk])):
+                q0, qn = QS[blk][i]
+                put(("Q", blk, i), "V", quantize, (blk, i),
+                    [("IL", blk, j0) for (j0, nj, eng) in PARTS[blk] if j0 < q0 + qn and j0 + nj > q0])
+                for k in range(qn):
+                    where[(blk, (q0 + k) % 4, (q0 + k) // 4)] = (i, k)
         for w in range(NW):
             for h in range(2):
                 put(("AT", w, h), "T", agg_transposes, (w, h) + AT_TAG[w], [], AT_TAG[w][0], AT_TAG[w][1], [("AE", w, h)])
@@ -259,7 +270,7 @@ def tile_stsindividuallayer_pb_kernel(tc, agg, W_bytes, W_scale, b, out):
             blk, j = divmod(s, 4)
             f = blk % NF
             for h in range(2):
-                put(("MM", s, h), "T", mm, (s, h), [("Q", blk, where[(blk, j, h)] // 4), ("AQ", blk // NF)],
+                put(("MM", s, h), "T", mm, (s, h), [("Q", blk, where[(blk, j, h)][0]), ("AQ", blk // NF)],
                     "LR%d" % h, LR_BUFS[h], [("SG", s) if h else ("PR", s)])
             put(("SG", s), "S", sigmoid, (s,), [("MM", s, 1), ("BC",)], "sig", SIG_BUFS, [("PR", s)])
             put(("PR", s), "V", product, (s,), [("MM", s, 0), ("SG", s)], "glu", GLU_BUFS, [("TR", s)])
@@ -267,46 +278,34 @@ def tile_stsindividuallayer_pb_kernel(tc, agg, W_bytes, W_scale, b, out):
             put(("MG", s), "V", merge, (s, "S" if s in CPS else "V"), [("TR", s)] + ([("MG", s - 4)] if f else []))
 
         V, S, G, T = queues["V"], queues["S"], queues["G"], queues["T"]
-        V.extend([("Wd", 0, 1), ("Wd", 0, 2), ("Wd", 0, 3), ("IL", 0, 0), ("IL", 0, 1), ("AE", 0, 0), ("AE", 0, 1), ("AQ", 0), ("Q", 0, 0),
-                  ("BC",), ("IL", 0, 2), ("IL", 0, 3), ("Q", 0, 1)])
+        V.extend([("Wd", 0, 1), ("Wd", 0, 2), ("Wd", 0, 3)] + HEAD_V)
         planes = [("Wd", blk, t) for blk in range(1, NB) for t in range(4) if WD[(blk, t)] == "S"]
         S.append(("Wd", 0, 0))
         S.extend(planes[:4 + AHEAD])
         planes = planes[4 + AHEAD:]
-        T.extend([("AT", 0, 0), ("AT", 0, 1), ("BT",), ("MM", 0, 1), ("MM", 0, 0), ("MM", 1, 1), ("MM", 1, 0), ("MM", 2, 1)])
+        T.extend([("AT", 0, 0), ("AT", 0, 1), ("BT",)] + NEXT_MM(0))
         for c in range(NB - 1):
             s0 = 4 * c
             if c + 1 < NB:
                 G.extend([("IL", c + 1, j0) for (j0, nj, e) in PARTS[c + 1] if e == "G"])
-            early = [("MG", s) for s in (s0 - 3, s0 - 2, s0 - 1) if s in CPS]
-            sgs = [("SG", s0 + j) for j in range(4)]
-            S.extend(SORDER(sgs, early) if early else sgs)
-            fill = planes[:4]
+            S.extend([("SG", s0 + j) for j in range(4)])
+            S.extend(planes[:4])
             planes = planes[4:]
             if c + 1 < NB:
-                fill = fill[:IL_AT] + [("IL", c + 1, j0) for (j0, nj, e) in PARTS[c + 1] if e == "S"] + fill[IL_AT:]
-            own = [("MG", s0)] if s0 in CPS else []
-            if c == 0 and AE[1] == "S":
-                own = [("AE", 1, 0), ("AE", 1, 1)] + own
-            k = OWN_AFTER
-            S.extend(fill[:k] + own + fill[k:])
-            vq = []
+                S.extend([("IL", c + 1, j0) for (j0, nj, e) in PARTS[c + 1] if e == "S"])
             if c > 0:
-                vq.extend([("MG", s0 - 3), ("PR", s0 - 1), ("MG", s0 - 2)])
-            vq.extend([("PR", s0), ("PR", s0 + 1), ("PR", s0 + 2)])
+                V.extend([("MG", s0 - 3), ("PR", s0 - 1), ("MG", s0 - 2)])
+            V.extend([("PR", s0), ("PR", s0 + 1), ("PR", s0 + 2)])
             if c > 0:
-                vq.append(("MG", s0 - 1))
-            elif AE[1] == "V":
-                vq.extend([("AE", 1, 0), ("AE", 1, 1)])
-            vq.append(("MG", s0))
-            V.extend([x for x in vq if x[0] != "MG" or x[1] not in CPS])
+                V.append(("MG", s0 - 1))
+            else:
+                V.extend([("AE", 1, 0), ("AE", 1, 1)])
+            V.append(("MG", s0))
             if c == 1:
                 V.append(("AQ", 1))
             if c + 1 < NB:
                 V.extend([("IL", c + 1, j0) for (j0, nj, e) in PARTS[c + 1] if e == "V"])
-                V.extend([("Q", c + 1, 0), ("Q", c + 1, 1)])
-            if c + 2 < NB:
-                V.extend([("Wd", c + 2, t) for t in range(4) if WD[(c + 2, t)] == "V"])
+                V.extend([("Q", c + 1, 1), ("Q", c + 1, 0)])
             T.extend([("MM", s0 + 3, 1), ("MM", s0 + 2, 0)])
             if c > 0:
                 T.append(("TR", s0 - 1))
@@ -314,7 +313,7 @@ def tile_stsindividuallayer_pb_kernel(tc, agg, W_bytes, W_scale, b, out):
                 T.extend([("AT", 1, 0), ("AT", 1, 1)])
             T.extend([("TR", s0), ("MM", s0 + 3, 0), ("TR", s0 + 1), ("TR", s0 + 2)])
             if c + 1 < NB:
-                T.extend([("MM", s0 + 4, 1), ("MM", s0 + 4, 0), ("MM", s0 + 5, 1), ("MM", s0 + 5, 0), ("MM", s0 + 6, 1)])
+                T.extend(NEXT_MM(s0 + 4))
         S.extend([("SG", 20), ("SG", 21), ("SG", 22), ("SG", 23)])
         V.extend([("MG", 17), ("PR", 19), ("MG", 18), ("PR", 20), ("PR", 21), ("PR", 22), ("MG", 19), ("PR", 23), ("MG", 20), ("MG", 21), ("MG", 22), ("MG", 23)])
         T.extend([("MM", 23, 1), ("MM", 22, 0), ("TR", 19), ("TR", 20), ("MM", 23, 0), ("TR", 21), ("TR", 22), ("TR", 23)])

@@ -95,7 +95,7 @@ def tile_stsindividuallayer_pb_kernel(tc, agg, W_bytes, W_scale, b, out):
                 grp[(blk, hh)] = work.tile([P, 16 * P], BF16, tag="grp%d" % hh, bufs=GRP_BUFS, name="grp%d_%d" % (blk, hh), align_bytes=64)
             src = wide[blk][:, :, P * s0:P * (s0 + ns)]
             dst = grp[(blk, hh)][:, 4 * P * (s0 - 4 * hh):4 * P * (s0 - 4 * hh + ns)]
-            if FAST:
+            if eng in FAST:
                 src = src.rearrange("p t (c i) -> p c t i", i=4)
                 dst = dst.rearrange("p (c i t) -> p c t i", i=4, t=4)
             else:
@@ -219,7 +219,7 @@ def tile_stsindividuallayer_pb_kernel(tc, agg, W_bytes, W_scale, b, out):
 
         GRP_BUFS, T_BUFS, SIG_BUFS, GLU_BUFS = 1, 2, 6, 4
         LR_BUFS = (3, 3)
-        FAST = False
+        FAST = ("V", "S")
         WD = {(blk, t): "S" for blk in range(NB) for t in range(4)}
         for t in (1, 2, 3):
             WD[(0, t)] = "V"

@@ -223,7 +223,7 @@ def tile_stsindividuallayer_pb_kernel(tc, agg, W_bytes, W_scale, b, out):
         WD = {(blk, t): "S" for blk in range(NB) for t in range(4)}
         for t in (1, 2, 3):
             WD[(0, t)] = "V"
-        PARTS = {blk: [(4, 4, "G"), (2, 2, "G"), (0, 2, "V")] for blk in range(NB)}
+        PARTS = {blk: [(4, 4, "G"), (1, 3, "G"), (0, 1, "V")] for blk in range(NB)}
         PARTS[0] = [(4, 2, "V"), (0, 2, "V"), (6, 2, "V"), (2, 2, "V")]
         PARTS[NB - 1] = [(4, 4, "G"), (2, 2, "G"), (0, 2, "S")]
         AT_TAG = {0: ("T", 2), 1: ("LR1", 3)}

@@ -224,12 +224,13 @@ def tile_stsindividuallayer_pb_kernel(tc, agg, W_bytes, W_scale, b, out):
         for t in (1, 2, 3):
             WD[(0, t)] = "V"
         PARTS = {blk: [(4, 4, "G"), (1, 3, "G"), (0, 1, "V")] for blk in range(NB)}
+        PARTS[1] = [(4, 4, "G"), (2, 2, "G"), (0, 2, "V")]
         PARTS[0] = [(4, 2, "V"), (0, 2, "V"), (6, 2, "V"), (2, 2, "V")]
         PARTS[NB - 1] = [(4, 4, "G"), (2, 2, "G"), (0, 2, "S")]
         AT_TAG = {0: ("T", 2), 1: ("LR1", 3)}
         AE = {0: "V", 1: "V"}
         BC = "V"
-        CPS = ()
+        CPS = (15,)
         AHEAD = 1
         HEAD_V = [("IL", 0, 4), ("IL", 0, 0), ("AE", 0, 0), ("AE", 0, 1), ("AQ", 0), ("Q", 0, 0), ("Q", 0, 1), ("BC",), ("IL", 0, 6), ("IL", 0, 2), ("Q", 0, 2), ("Q", 0, 3)]
         NEXT_MM = lambda s: ([("MM", s, 1), ("MM", s + 1, 1), ("MM", s + 2, 1), ("MM", s, 0), ("MM", s + 1, 0)] if s else [("MM", 0, 1), ("MM", 1, 1), ("MM", 0, 0), ("MM", 1, 0), ("MM", 2, 1)])
@@ -317,6 +318,8 @@ def tile_stsindividuallayer_pb_kernel(tc, agg, W_bytes, W_scale, b, out):
         S.extend([("SG", 20), ("SG", 21), ("SG", 22), ("SG", 23)])
         V.extend([("MG", 17), ("PR", 19), ("MG", 18), ("PR", 20), ("PR", 21), ("PR", 22), ("MG", 19), ("PR", 23), ("MG", 20), ("MG", 21), ("MG", 22), ("MG", 23)])
         T.extend([("MM", 23, 1), ("MM", 22, 0), ("TR", 19), ("TR", 20), ("MM", 23, 0), ("TR", 21), ("TR", 22), ("TR", 23)])
+        V.remove(("MG", 15))
+        S.insert(S.index(("SG", 19)) + 1, ("MG", 15))
         done = set()
         handed = {}
 

@@ -195,6 +195,20 @@ def tile_stsindividuallayer_pb_kernel(tc, agg, W_bytes, W_scale, b, out):
             )
             glu[s] = g
 
+        val = {}
+
+        def value_out(s):
+            blk, j = divmod(s, 4)
+            v = work.tile([P, N], F32, tag="val", bufs=2, name="val%d" % s)
+            col = blk * 8 + j
+            nc.scalar.activation(out=v[:], in_=acc[(s, 0)][:], func=ACT.Identity, bias=bias[:, col:col + 1])
+            val[s] = v
+
+        def product_g(s):
+            g = work.tile([P, N], F32, tag="glu", bufs=GLU_BUFS, name="glu%d" % s)
+            nc.gpsimd.tensor_tensor(out=g[:], in0=val[s][:], in1=sig[s][:], op=ALU.mult)
+            glu[s] = g
+
         def turn(s):
             gt = psum.tile([P, 4, P], F32, tag=T_TAG(s)[0], bufs=T_TAG(s)[1], name="gt%d" % s)
             for i in range(4):
@@ -224,7 +238,7 @@ def tile_stsindividuallayer_pb_kernel(tc, agg, W_bytes, W_scale, b, out):
         for t in (1, 2, 3):
             WD[(0, t)] = "V"
         PARTS = {blk: [(4, 4, "G"), (1, 3, "G"), (0, 1, "V")] for blk in range(NB)}
-        PARTS[1] = [(4, 4, "G"), (2, 2, "G"), (0, 2, "V")]
+        PARTS[1] = [(4, 4, "G"), (2, 2, "G"), (1, 1, "V"), (0, 1, "S")]
         PARTS[0] = [(4, 2, "V"), (0, 2, "V"), (6, 2, "V"), (2, 2, "V")]
         PARTS[NB - 1] = [(4, 4, "G"), (2, 2, "G"), (0, 2, "S")]
         AT_TAG = {0: ("T", 2), 1: ("LR1", 3)}
@@ -274,7 +288,12 @@ def tile_stsindividuallayer_pb_kernel(tc, agg, W_bytes, W_scale, b, out):
                 put(("MM", s, h), "T", mm, (s, h), [("Q", blk, where[(blk, j, h)][0]), ("AQ", blk // NF)],
                     "LR%d" % h, LR_BUFS[h], [("SG", s) if h else ("PR", s)])
             put(("SG", s), "S", sigmoid, (s,), [("MM", s, 1), ("BC",)], "sig", SIG_BUFS, [("PR", s)])
-            put(("PR", s), "V", product, (s,), [("MM", s, 0), ("SG", s)], "glu", GLU_BUFS, [("TR", s)])
+            if s in (19,):
+                ops[("MM", s, 0)] = ops[("MM", s, 0)][:5] + ([("ID", s)],)
+                put(("ID", s), "S", value_out, (s,), [("MM", s, 0), ("BC",)], "val", 2, [("PR", s)])
+                put(("PR", s), "G", product_g, (s,), [("ID", s), ("SG", s)], "glu", GLU_BUFS, [("TR", s)])
+            else:
+                put(("PR", s), "V", product, (s,), [("MM", s, 0), ("SG", s)], "glu", GLU_BUFS, [("TR", s)])
             put(("TR", s), "T", turn, (s,), [("PR", s)], T_TAG(s)[0], T_TAG(s)[1], [("MG", s)])
             put(("MG", s), "V", merge, (s, "S" if s in CPS else "V"), [("TR", s)] + ([("MG", s - 4)] if f else []))
 
@@ -290,9 +309,11 @@ def tile_stsindividuallayer_pb_kernel(tc, agg, W_bytes, W_scale, b, out):
             if c + 1 < NB:
                 G.extend([("IL", c + 1, j0) for (j0, nj, e) in PARTS[c + 1] if e == "G"])
             S.extend([("SG", s0 + j) for j in range(4)])
+            if c == 0:
+                S.insert(S.index(("SG", 2)), ("IL", 1, 0))
             S.extend(planes[:4])
             planes = planes[4:]
-            if c + 1 < NB:
+            if c > 0:
                 S.extend([("IL", c + 1, j0) for (j0, nj, e) in PARTS[c + 1] if e == "S"])
             if c > 0:
                 V.extend([("MG", s0 - 3), ("PR", s0 - 1), ("MG", s0 - 2)])
@@ -315,8 +336,9 @@ def tile_stsindividuallayer_pb_kernel(tc, agg, W_bytes, W_scale, b, out):
             T.extend([("TR", s0), ("MM", s0 + 3, 0), ("TR", s0 + 1), ("TR", s0 + 2)])
             if c + 1 < NB:
                 T.extend(NEXT_MM(s0 + 4))
-        S.extend([("SG", 20), ("SG", 21), ("SG", 22), ("SG", 23)])
-        V.extend([("MG", 17), ("PR", 19), ("MG", 18), ("PR", 20), ("PR", 21), ("PR", 22), ("MG", 19), ("PR", 23), ("MG", 20), ("MG", 21), ("MG", 22), ("MG", 23)])
+        S.extend([("ID", 19), ("SG", 20), ("SG", 21), ("SG", 22), ("SG", 23)])
+        V.extend([("MG", 17), ("MG", 18), ("PR", 20), ("PR", 21), ("PR", 22), ("MG", 19), ("PR", 23), ("MG", 20), ("MG", 21), ("MG", 22), ("MG", 23)])
+        G.extend([("PR", 19)])
         T.extend([("MM", 23, 1), ("MM", 22, 0), ("TR", 19), ("TR", 20), ("MM", 23, 0), ("TR", 21), ("TR", 22), ("TR", 23)])
         V.remove(("MG", 15))
         S.insert(S.index(("SG", 19)) + 1, ("MG", 15))

@@ -26,6 +26,8 @@ def tile_stsindividuallayer_pb_kernel(tc, agg, W_bytes, W_scale, b, out):
         psum = ctx.enter_context(tc.psum_pool(name="psum", bufs=2))
         ctx.enter_context(tc.manual_schedule())
 
+        sc = keep.tile([P, 4], F32, name="sc")
+        nc.scalar.dma_start(out=sc[:], in_=W_scale[0, 0].rearrange("(p t) d -> p (t d)", t=4))
         zero = keep.tile([P, 1], F32, name="zero")
         nc.vector.memset(zero[:], 0.0)
         warm = keep.tile([P, 1], F32, name="warm")
@@ -37,8 +39,6 @@ def tile_stsindividuallayer_pb_kernel(tc, agg, W_bytes, W_scale, b, out):
         ident_b = keep.tile([P, P], BF16, name="ident_b")
         make_identity(nc, ident_b[:])
 
-        sc = keep.tile([P, 4], F32, name="sc")
-        nc.sync.dma_start(out=sc[:], in_=W_scale[0, 0].rearrange("(p t) d -> p (t d)", t=4))
         wbytes = {}
 
         def load_plane(blk, t):
@@ -239,14 +239,14 @@ def tile_stsindividuallayer_pb_kernel(tc, agg, W_bytes, W_scale, b, out):
             WD[(0, t)] = "V"
         PARTS = {blk: [(4, 4, "G"), (1, 3, "G"), (0, 1, "V")] for blk in range(NB)}
         PARTS[1] = [(4, 4, "G"), (2, 2, "G"), (1, 1, "V"), (0, 1, "S")]
-        PARTS[0] = [(4, 2, "V"), (0, 2, "V"), (6, 2, "V"), (2, 2, "V")]
+        PARTS[0] = [(4, 2, "V"), (0, 2, "G"), (6, 2, "V"), (2, 2, "V")]
         PARTS[NB - 1] = [(4, 4, "G"), (2, 2, "G"), (0, 2, "S")]
         AT_TAG = {0: ("T", 2), 1: ("LR1", 3)}
         AE = {0: "V", 1: "V"}
         BC = "V"
         CPS = (15,)
         AHEAD = 1
-        HEAD_V = [("IL", 0, 4), ("IL", 0, 0), ("AE", 0, 0), ("AE", 0, 1), ("AQ", 0), ("Q", 0, 0), ("Q", 0, 1), ("BC",), ("IL", 0, 6), ("IL", 0, 2), ("Q", 0, 2), ("Q", 0, 3)]
+        HEAD_V = [("IL", 0, 4), ("AE", 0, 0), ("AE", 0, 1), ("Q", 0, 0), ("AQ", 0), ("Q", 0, 1), ("BC",), ("IL", 0, 6), ("IL", 0, 2), ("Q", 0, 2), ("Q", 0, 3)]
         NEXT_MM = lambda s: ([("MM", s, 1), ("MM", s + 1, 1), ("MM", s + 2, 1), ("MM", s, 0), ("MM", s + 1, 0)] if s else [("MM", 0, 1), ("MM", 1, 1), ("MM", 0, 0), ("MM", 1, 0), ("MM", 2, 1)])
         QS = {blk: [(0, 4), (4, 4)] for blk in range(NB)}
         QS[0] = [(4, 2), (0, 2), (6, 2), (2, 2)]
@@ -303,6 +303,7 @@ def tile_stsindividuallayer_pb_kernel(tc, agg, W_bytes, W_scale, b, out):
         S.append(("Wd", 0, 0))
         S.extend(planes[:4 + AHEAD])
         planes = planes[4 + AHEAD:]
+        G.append(("IL", 0, 0))
         T.extend([("AT", 0, 0), ("AT", 0, 1), ("BT",)] + NEXT_MM(0))
         for c in range(NB - 1):
             s0 = 4 * c

@@ -54,7 +54,7 @@ def tile_stsindividuallayer_pb_kernel(tc, agg, W_bytes, W_scale, b, out):
 
         def load_agg(w):
             a = keep.tile([P, 4, C], BF16, name="a_sb%d" % w)
-            nc.sync.dma_start(out=a[:], in_=agg[0, w].rearrange("(i p) k -> p i k", p=P))
+            nc.sync.dma_start(out=a[:], in_=agg[0, w].rearrange("(p i) k -> p i k", i=4))
             a_sb.append(a)
 
         def load_w(blk):
@@ -228,7 +228,7 @@ def tile_stsindividuallayer_pb_kernel(tc, agg, W_bytes, W_scale, b, out):
                 nc.vector.tensor_tensor(out=bestT[(w, j)][:], in0=gluT[s][:], in1=bestT[(w, j)][:], op=ALU.max)
             if f == NF - 1:
                 nc.sync.dma_start(
-                    out=out[0, w].rearrange("(i p) c -> p i c", p=P)[:, :, P * j:P * (j + 1)], in_=bestT[(w, j)][:]
+                    out=out[0, w].rearrange("(p i) c -> p i c", i=4)[:, :, P * j:P * (j + 1)], in_=bestT[(w, j)][:]
                 )
 
         GRP_BUFS, T_BUFS, SIG_BUFS, GLU_BUFS = 1, 2, 6, 4

@@ -250,7 +250,7 @@ def tile_stsindividuallayer_pb_kernel(tc, agg, W_bytes, W_scale, b, out):
         NEXT_MM = lambda s: ([("MM", s, 1), ("MM", s + 1, 1), ("MM", s + 2, 1), ("MM", s, 0), ("MM", s + 1, 0)] if s else [("MM", 0, 1), ("MM", 1, 1), ("MM", 0, 0), ("MM", 1, 0), ("MM", 2, 1)])
         QS = {blk: [(0, 4), (4, 4)] for blk in range(NB)}
         QS[0] = [(4, 2), (0, 2), (6, 2), (2, 2)]
-        T_TAG = lambda s: ("LR1", 3) if s in (21, 23) else ("T", 2)
+        T_TAG = lambda s: ("LR1", 3) if s in (19, 22, 23) else ("T", 2)
         ops = {}
         where = {}
         queues = {"V": [], "S": [], "G": [], "T": []}
@@ -309,10 +309,13 @@ def tile_stsindividuallayer_pb_kernel(tc, agg, W_bytes, W_scale, b, out):
             s0 = 4 * c
             if c + 1 < NB:
                 G.extend([("IL", c + 1, j0) for (j0, nj, e) in PARTS[c + 1] if e == "G"])
-            S.extend([("SG", s0 + j) for j in range(4)])
+            S.extend([("SG", s0 + j) for j in range(3)])
             if c == 0:
                 S.insert(S.index(("SG", 2)), ("IL", 1, 0))
-            S.extend(planes[:4])
+            late = 3 if 0 < c < 4 else 0
+            S.extend(planes[:late])
+            S.append(("SG", s0 + 3))
+            S.extend(planes[late:4])
             planes = planes[4:]
             if c > 0:
                 S.extend([("IL", c + 1, j0) for (j0, nj, e) in PARTS[c + 1] if e == "S"])
@@ -338,7 +341,7 @@ def tile_stsindividuallayer_pb_kernel(tc, agg, W_bytes, W_scale, b, out):
             if c + 1 < NB:
                 T.extend(NEXT_MM(s0 + 4))
         S.extend([("ID", 19), ("SG", 20), ("SG", 21), ("SG", 22), ("SG", 23)])
-        V.extend([("MG", 17), ("MG", 18), ("PR", 20), ("PR", 21), ("PR", 22), ("MG", 19), ("PR", 23), ("MG", 20), ("MG", 21), ("MG", 22), ("MG", 23)])
+        V.extend([("MG", 17), ("MG", 18), ("PR", 20), ("PR", 21), ("PR", 22), ("MG", 20), ("PR", 23), ("MG", 21), ("MG", 19), ("MG", 22), ("MG", 23)])
         G.extend([("PR", 19)])
         T.extend([("MM", 23, 1), ("MM", 22, 0), ("TR", 19), ("TR", 20), ("MM", 23, 0), ("TR", 21), ("TR", 22), ("TR", 23)])
         V.remove(("MG", 15))

from contextlib import ExitStack

import concourse.mybir as mybir
from concourse.masks import make_identity

F32 = mybir.dt.float32
BF16 = mybir.dt.bfloat16
U32 = mybir.dt.uint32
U8 = mybir.dt.uint8
FP8 = mybir.dt.float8_e4m3fn
X4 = mybir.dt.float8_e4m3fn_x4
ACT = mybir.ActivationFunctionType
ALU = mybir.AluOpType

P = 128
NW, NF, N, C = 2, 3, 512, 512
NB = NW * NF
FLOPS = 2 * NW * NF * N * C * 2 * C


def tile_stsindividuallayer_pb_kernel(tc, agg, W_bytes, W_scale, b, out):
    nc = tc.nc
    with ExitStack() as ctx:
        keep = ctx.enter_context(tc.tile_pool(name="keep", bufs=1))
        work = ctx.enter_context(tc.tile_pool(name="work", bufs=3))
        psum = ctx.enter_context(tc.psum_pool(name="psum", bufs=2))
        ctx.enter_context(tc.manual_schedule())

        sc = keep.tile([P, 4], F32, name="sc")
        nc.scalar.dma_start(out=sc[:], in_=W_scale[0, 0].rearrange("(p t) d -> p (t d)", t=4))
        zero = keep.tile([P, 1], F32, name="zero")
        nc.vector.memset(zero[:], 0.0)
        warm = keep.tile([P, 1], F32, name="warm")
        nc.scalar.activation(out=warm[:], in_=zero[:], func=ACT.Sigmoid)
        b_rows = keep.tile([P, P], BF16, name="b_rows")
        nc.gpsimd.memset(b_rows[:], 0.0)
        ident_f = keep.tile([P, P], F32, name="ident_f")
        make_identity(nc, ident_f[:])
        ident_b = keep.tile([P, P], BF16, name="ident_b")
        make_identity(nc, ident_b[:])

        wbytes = {}

        def load_plane(blk, t):
            w, f = divmod(blk, NF)
            wb = keep.tile([P, 2 * C], U8, name="wbytes%d_%d" % (blk, t))
            nc.sync.dma_start(out=wb[:], in_=W_bytes[w, f].rearrange("(p t) n -> p t n", t=4)[:, t, :])
            wbytes[(blk, t)] = wb[:]

        for t in (1, 0, 2, 3):
            load_plane(0, t)
        load_plane(1, 0)
        a_sb = []

        def load_agg(w):
            a = keep.tile([P, 4, C], BF16, name="a_sb%d" % w)
            nc.sync.dma_start(out=a[:], in_=agg[0, w].rearrange("(p i) k -> p i k", i=4))
            a_sb.append(a)

        def load_w(blk):
            w, f = divmod(blk, NF)
            wb = keep.tile([P, 4, 2 * C], U8, name="wbytes%d" % blk)
            nc.sync.dma_start(out=wb[:], in_=W_bytes[w, f].rearrange("(p t) n -> p t n", t=4))
            for t in range(4):
                wbytes[(blk, t)] = wb[:, t, :]

        load_agg(0)
        for t in (1, 2, 3):
            load_plane(1, t)
        nc.sync.dma_start(out=b_rows[0:48, :], in_=b.rearrange("w f (c p) -> (w f c) p", p=P))
        load_w(2)
        load_agg(1)
        load_w(3)
        load_w(4)
        load_w(5)

        wide = {}

        def widen(blk, t, eng):
            if blk not in wide:
                wide[blk] = keep.tile([P, 4, 2 * C], BF16, name="wide%d" % blk)
            src = wbytes[(blk, t)].bitcast(FP8)
            dst = wide[blk][:, t, :]
            if eng == "S":
                nc.scalar.activation(out=dst, in_=src, func=ACT.Copy, scale=sc[:, t:t + 1])
            else:
                nc.vector.tensor_scalar(out=dst, in0=src, scalar1=sc[:, t:t + 1], scalar2=None, op0=ALU.mult)

        grp = {}
        half = {}

        def interleave(blk, s0, ns, eng):
            hh = s0 // 4
            if (blk, hh) not in grp:
                grp[(blk, hh)] = work.tile([P, 16 * P], BF16, tag="grp%d" % hh, bufs=GRP_BUFS, name="grp%d_%d" % (blk, hh), align_bytes=64)
            src = wide[blk][:, :, P * s0:P * (s0 + ns)]
            dst = grp[(blk, hh)][:, 4 * P * (s0 - 4 * hh):4 * P * (s0 - 4 * hh + ns)]
            if eng in FAST:
                src = src.rearrange("p t (c i) -> p c t i", i=4)
                dst = dst.rearrange("p (c i t) -> p c t i", i=4, t=4)
            else:
                src = src.rearrange("p t x -> p x t")
                dst = dst.rearrange("p (x t) -> p x t", t=4)
            if eng == "G":
                nc.gpsimd.tensor_scalar(out=dst, in0=src, scalar1=1.0, scalar2=0.0, op0=ALU.mult, op1=ALU.add)
            elif eng == "S":
                nc.scalar.copy(out=dst, in_=src)
            else:
                nc.vector.tensor_copy(out=dst, in_=src)

        def quantize(blk, i):
            s0, ns = QS[blk][i]
            cd = keep.tile([P, ns * P], U32, name="wc%d_%d" % (blk, i), align_bytes=64)
            sl = keep.tile([P, ns * P], U8, name="ws%d_%d" % (blk, i), align_bytes=64)
            nc.vector.quantize_mx(out=cd[:].bitcast(X4), scales=sl[:], in_=grp[(blk, s0 // 4)][:, 4 * P * (s0 % 4):4 * P * (s0 % 4 + ns)])
            half[(blk, i)] = (cd, sl)

        a_grp = {}
        a_q = {}
        xts = {}

        def agg_transposes(w, h, tag, bufs):
            if w not in a_grp:
                a_grp[w] = keep.tile([P, 4 * N], BF16, name="a_grp%d" % w, align_bytes=64)
            xt = psum.tile([P, 2, 2, P], F32, tag=tag, bufs=bufs, name="xt%d_%d" % (w, h))
            for i2 in range(2):
                words = a_sb[w][:, 2 * h + i2, :].bitcast(F32)
                for u in range(2):
                    nc.tensor.transpose(xt[:, i2, u, :], words[:, u:C // 2:2], ident_f[:])
            xts[(w, h)] = xt

        def agg_evac(w, h, eng):
            dst = a_grp[w][:].bitcast(F32)[:, 512 * h:512 * (h + 1)].rearrange("p (i r u) -> p i r u", i=2, u=2)
            src = xts[(w, h)][:].rearrange("p i u r -> p i r u")
            if eng == "S":
                nc.scalar.copy(out=dst, in_=src)
            else:
                nc.vector.tensor_copy(out=dst, in_=src)

        def agg_quantize(w):
            cd = keep.tile([P, N], U32, name="ac%d" % w, align_bytes=64)
            sl = keep.tile([P, N], U8, name="as%d" % w, align_bytes=64)
            nc.vector.quantize_mx(out=cd[:].bitcast(X4), scales=sl[:], in_=a_grp[w][:])
            a_q[w] = (cd, sl)

        bias = keep.tile([P, 48], F32, name="bias")
        bTs = []

        def bias_turn():
            bT = psum.tile([P, P], BF16, tag="T", bufs=T_BUFS, name="bT")
            nc.tensor.transpose(bT[:], b_rows[:], ident_b[:])
            bTs.append(bT)

        def bias_copy(eng):
            if eng == "S":
                nc.scalar.copy(out=bias[:], in_=bTs[0][:, 0:48])
            else:
                nc.vector.tensor_copy(out=bias[:], in_=bTs[0][:, 0:48])

        acc = {}

        def mm(s, h):
            blk, j = divmod(s, 4)
            w = blk // NF
            ps = psum.tile([P, N], F32, tag="LR%d" % h, bufs=LR_BUFS[h], name="acc%d_%d" % (s, h))
            i, k = where[(blk, j, h)]
            cd, sl = half[(blk, i)]
            cols = slice(k * P, (k + 1) * P)
            nc.tensor.matmul_mx(
                out=ps[:], lhsT=cd[:, cols].bitcast(X4), lhsT_scale=sl[:, cols],
                rhs=a_q[w][0][:].bitcast(X4), rhs_scale=a_q[w][1][:],
                start=True, stop=True,
            )
            acc[(s, h)] = ps

        sig = {}
        glu = {}
        bestT = {}
        gluT = {}

        def sigmoid(s):
            blk, j = divmod(s, 4)
            sg = work.tile([P, N], F32, tag="sig", bufs=SIG_BUFS, name="sig%d" % s)
            col = blk * 8 + 4 + j
            nc.scalar.activation(out=sg[:], in_=acc[(s, 1)][:], func=ACT.Sigmoid, bias=bias[:, col:col + 1])
            sig[s] = sg

        def product(s):
            blk, j = divmod(s, 4)
            g = work.tile([P, N], F32, tag="glu", bufs=GLU_BUFS, name="glu%d" % s)
            col = blk * 8 + j
            nc.vector.scalar_tensor_tensor(
                out=g[:], in0=acc[(s, 0)][:], scalar=bias[:, col:col + 1], in1=sig[s][:],
                op0=ALU.add, op1=ALU.mult,
            )
            glu[s] = g

        val = {}

        def value_out(s):
            blk, j = divmod(s, 4)
            v = work.tile([P, N], F32, tag="val", bufs=2, name="val%d" % s)
            col = blk * 8 + j
            nc.scalar.activation(out=v[:], in_=acc[(s, 0)][:], func=ACT.Identity, bias=bias[:, col:col + 1])
            val[s] = v

        def product_g(s):
            g = work.tile([P, N], F32, tag="glu", bufs=GLU_BUFS, name="glu%d" % s)
            nc.gpsimd.tensor_tensor(out=g[:], in0=val[s][:], in1=sig[s][:], op=ALU.mult)
            glu[s] = g

        def turn(s):
            gt = psum.tile([P, 4, P], F32, tag=T_TAG(s)[0], bufs=T_TAG(s)[1], name="gt%d" % s)
            for i in range(4):
                nc.tensor.transpose(gt[:, i, :], glu[s][:, P * i:P * (i + 1)], ident_f[:])
            gluT[s] = gt

        def merge(s, eng):
            blk, j = divmod(s, 4)
            w, f = divmod(blk, NF)
            if f == 0:
                bestT[(w, j)] = keep.tile([P, 4, P], F32, name="bestT%d_%d" % (w, j))
                if eng == "S":
                    nc.scalar.copy(out=bestT[(w, j)][:], in_=gluT[s][:])
                else:
                    nc.vector.tensor_copy(out=bestT[(w, j)][:], in_=gluT[s][:])
            else:
                nc.vector.tensor_tensor(out=bestT[(w, j)][:], in0=gluT[s][:], in1=bestT[(w, j)][:], op=ALU.max)
            if f == NF - 1:
                nc.sync.dma_start(
                    out=out[0, w].rearrange("(p i) c -> p i c", i=4)[:, :, P * j:P * (j + 1)], in_=bestT[(w, j)][:]
                )

        GRP_BUFS, T_BUFS, SIG_BUFS, GLU_BUFS = 1, 2, 6, 4
        LR_BUFS = (3, 3)
        FAST = ("V", "S")
        WD = {(blk, t): "S" for blk in range(NB) for t in range(4)}
        for t in (1, 2, 3):
            WD[(0, t)] = "V"
        PARTS = {blk: [(4, 4, "G"), (1, 3, "G"), (0, 1, "V")] for blk in range(NB)}
        PARTS[1] = [(4, 4, "G"), (2, 2, "G"), (1, 1, "V"), (0, 1, "S")]
        PARTS[0] = [(4, 2, "V"), (0, 2, "G"), (6, 2, "V"), (2, 2, "V")]
        PARTS[NB - 1] = [(4, 4, "G"), (2, 2, "G"), (0, 2, "S")]
        AT_TAG = {0: ("T", 2), 1: ("LR1", 3)}
        AE = {0: "V", 1: "V"}
        BC = "V"
        CPS = (15,)
        AHEAD = 1
        HEAD_V = [("IL", 0, 4), ("AE", 0, 0), ("AE", 0, 1), ("Q", 0, 0), ("AQ", 0), ("Q", 0, 1), ("BC",), ("IL", 0, 6), ("IL", 0, 2), ("Q", 0, 2), ("Q", 0, 3)]
        NEXT_MM = lambda s: ([("MM", s, 1), ("MM", s + 1, 1), ("MM", s + 2, 1), ("MM", s, 0), ("MM", s + 1, 0)] if s else [("MM", 0, 1), ("MM", 1, 1), ("MM", 0, 0), ("MM", 1, 0), ("MM", 2, 1)])
        QS = {blk: [(0, 4), (4, 4)] for blk in range(NB)}
        QS[0] = [(4, 2), (0, 2), (6, 2), (2, 2)]
        T_TAG = lambda s: ("LR1", 3) if s in (19, 22, 23) else ("T", 2)
        ops = {}
        where = {}
        queues = {"V": [], "S": [], "G": [], "T": []}

        def put(name, eng, fn, args, needs, tag=None, bufs=0, users=()):
            ops[name] = (fn, args, needs, tag, bufs, users)

        for blk in range(NB):
            for t in range(4):
                put(("Wd", blk, t), WD[(blk, t)], widen, (blk, t, WD[(blk, t)]), [])
            seen = set()
            for (j0, nj, eng) in PARTS[blk]:
                put(("IL", blk, j0), eng, interleave, (blk, j0, nj, eng),
                    [("Wd", blk, t) for t in range(4)] + [("IL", blk - 1, x[0]) for x in PARTS.get(blk - 1, []) if x[0] // 4 == j0 // 4],
                    None if j0 // 4 in seen else "grp%d" % (j0 // 4), GRP_BUFS,
                    [("Q", blk, i) for i in range(len(QS[blk])) if QS[blk][i][0] // 4 == j0 // 4])
                seen.add(j0 // 4)
            for i in range(len(QS[blk])):
                q0, qn = QS[blk][i]
                put(("Q", blk, i), "V", quantize, (blk, i),
                    [("IL", blk, j0) for (j0, nj, eng) in PARTS[blk] if j0 < q0 + qn and j0 + nj > q0])
                for k in range(qn):
                    where[(blk, (q0 + k) % 4, (q0 + k) // 4)] = (i, k)
        for w in range(NW):
            for h in range(2):
                put(("AT", w, h), "T", agg_transposes, (w, h) + AT_TAG[w], [], AT_TAG[w][0], AT_TAG[w][1], [("AE", w, h)])
                put(("AE", w, h), AE[w], agg_evac, (w, h, AE[w]), [("AT", w, h)])
            put(("AQ", w), "V", agg_quantize, (w,), [("AE", w, 0), ("AE", w, 1)])
        put(("BT",), "T", bias_turn, (), [], "T", T_BUFS, [("BC",)])
        put(("BC",), BC, bias_copy, (BC,), [("BT",)])
        for s in range(4 * NB):
            blk, j = divmod(s, 4)
            f = blk % NF
            for h in range(2):
                put(("MM", s, h), "T", mm, (s, h), [("Q", blk, where[(blk, j, h)][0]), ("AQ", blk // NF)],
                    "LR%d" % h, LR_BUFS[h], [("SG", s) if h else ("PR", s)])
            put(("SG", s), "S", sigmoid, (s,), [("MM", s, 1), ("BC",)], "sig", SIG_BUFS, [("PR", s)])
            if s in (19,):
                ops[("MM", s, 0)] = ops[("MM", s, 0)][:5] + ([("ID", s)],)
                put(("ID", s), "S", value_out, (s,), [("MM", s, 0), ("BC",)], "val", 2, [("PR", s)])
                put(("PR", s), "G", product_g, (s,), [("ID", s), ("SG", s)], "glu", GLU_BUFS, [("TR", s)])
            else:
                put(("PR", s), "V", product, (s,), [("MM", s, 0), ("SG", s)], "glu", GLU_BUFS, [("TR", s)])
            put(("TR", s), "T", turn, (s,), [("PR", s)], T_TAG(s)[0], T_TAG(s)[1], [("MG", s)])
            put(("MG", s), "V", merge, (s, "S" if s in CPS else "V"), [("TR", s)] + ([("MG", s - 4)] if f else []))

        V, S, G, T = queues["V"], queues["S"], queues["G"], queues["T"]
        V.extend([("Wd", 0, 1), ("Wd", 0, 2), ("Wd", 0, 3)] + HEAD_V)
        planes = [("Wd", blk, t) for blk in range(1, NB) for t in range(4) if WD[(blk, t)] == "S"]
        S.append(("Wd", 0, 0))
        S.extend(planes[:4 + AHEAD])
        planes = planes[4 + AHEAD:]
        G.append(("IL", 0, 0))
        T.extend([("AT", 0, 0), ("AT", 0, 1), ("BT",)] + NEXT_MM(0))
        for c in range(NB - 1):
            s0 = 4 * c
            if c + 1 < NB:
                G.extend([("IL", c + 1, j0) for (j0, nj, e) in PARTS[c + 1] if e == "G"])
            S.extend([("SG", s0 + j) for j in range(3)])
            if c == 0:
                S.insert(S.index(("SG", 2)), ("IL", 1, 0))
            late = 3 if 0 < c < 4 else 0
            S.extend(planes[:late])
            S.append(("SG", s0 + 3))
            S.extend(planes[late:4])
            planes = planes[4:]
            if c > 0:
                S.extend([("IL", c + 1, j0) for (j0, nj, e) in PARTS[c + 1] if e == "S"])
            if c > 0:
                V.extend([("MG", s0 - 3), ("PR", s0 - 1), ("MG", s0 - 2)])
            V.extend([("PR", s0), ("PR", s0 + 1), ("PR", s0 + 2)])
            if c > 0:
                V.append(("MG", s0 - 1))
            else:
                V.extend([("AE", 1, 0), ("AE", 1, 1)])
            V.append(("MG", s0))
            if c == 1:
                V.append(("AQ", 1))
            if c + 1 < NB:
                V.extend([("IL", c + 1, j0) for (j0, nj, e) in PARTS[c + 1] if e == "V"])
                V.extend([("Q", c + 1, 1), ("Q", c + 1, 0)])
            T.extend([("MM", s0 + 3, 1), ("MM", s0 + 2, 0)])
            if c > 0:
                T.append(("TR", s0 - 1))
            else:
                T.extend([("AT", 1, 0), ("AT", 1, 1)])
            T.extend([("TR", s0), ("MM", s0 + 3, 0), ("TR", s0 + 1), ("TR", s0 + 2)])
            if c + 1 < NB:
                T.extend(NEXT_MM(s0 + 4))
        S.extend([("ID", 19), ("SG", 20), ("SG", 21), ("SG", 22), ("SG", 23)])
        V.extend([("MG", 17), ("MG", 18), ("PR", 20), ("PR", 21), ("PR", 22), ("MG", 20), ("PR", 23), ("MG", 21), ("MG", 19), ("MG", 22), ("MG", 23)])
        G.extend([("PR", 19)])
        T.extend([("MM", 23, 1), ("MM", 22, 0), ("TR", 19), ("TR", 20), ("MM", 23, 0), ("TR", 21), ("TR", 22), ("TR", 23)])
        V.remove(("MG", 15))
        S.insert(S.index(("SG", 19)) + 1, ("MG", 15))
        done = set()
        handed = {}

        def ready(name):
            fn, args, needs, tag, bufs, users = ops[name]
            if any(x not in done for x in needs):
                return False
            if tag:
                lst = handed.setdefault(tag, [])
                if len(lst) >= bufs and any(x not in done for x in lst[len(lst) - bufs]):
                    return False
            return True

        at = {"T": 0, "S": 0, "V": 0, "G": 0}
        left = sum(len(queues[e]) for e in at)
        assert left == len(ops), (left, len(ops))
        while left:
            moved = 0
            for e in ("T", "S", "V", "G"):
                q = queues[e]
                while at[e] < len(q) and ready(q[at[e]]):
                    name = q[at[e]]
                    at[e] += 1
                    fn, args, needs, tag, bufs, users = ops[name]
                    if tag:
                        handed[tag].append(list(users))
                    fn(*args)
                    done.add(name)
                    moved += 1
            assert moved, [queues[e][at[e]] for e in at if at[e] < len(queues[e])]
            left -= moved
